import numpy as np
import ml_dtypes


def mxq(x, axis, fmt="e4m3"):
    dtype, down = {"e4m3": (ml_dtypes.float8_e4m3fn, 7), "e5m2": (ml_dtypes.float8_e5m2, 14)}[fmt]
    v = np.moveaxis(np.asarray(x, np.float32).astype(ml_dtypes.bfloat16).astype(np.float64), axis, -1)
    blocks = v.reshape(v.shape[:-1] + (-1, 32))
    amax = np.abs(blocks).max(-1, keepdims=True)
    byte = np.maximum(np.where(amax > 0, np.frexp(amax)[1] - 1 + 127, 0) - down, 1)
    scale = np.exp2(byte - 127.0)
    codes = (blocks / scale).astype(np.float32).astype(dtype).astype(np.float64)
    return np.moveaxis((codes * scale).reshape(v.shape), -1, axis)


WIDE = False


def mx_kscale(k):
    if not WIDE:
        return np.ones(k)
    levels = np.array([10, -10, 5, -5, 0])
    a = np.random.permutation(np.resize(levels, k // 512 * 4)).reshape(k // 512, 4)
    idx = np.arange(k)
    return np.exp2(a[idx // 512, idx % 128 // 32])


BF16 = ml_dtypes.bfloat16


def bf(x):
    return np.asarray(x, np.float32).astype(BF16)


def f64(x):
    return np.asarray(x).astype(np.float64)


B, C, OC, HH, WW, HEADS, RES, CPG = 4, 512, 256, 64, 64, 4, 16, 4
GROUPS = C // CPG
FH, FW = HH // RES, WW // RES
P = HH * WW
EPS = 1e-5


def setup_inputs():
    s = mx_kscale(C)
    g = np.random.standard_normal((B, GROUPS, CPG * P))
    g = g * (0.5 + np.random.random((B, GROUPS)))[:, :, None] + np.random.standard_normal((B, GROUPS))[:, :, None]
    return {"X": bf(g.reshape(B, C, HH, WW)),
            "gn_w": bf((1.0 + 0.1 * np.random.standard_normal(C)) * s),
            "gn_b": bf(0.1 * np.random.standard_normal(C) * s),
            "kqv_w": bf(np.random.standard_normal((OC, C)) * 2.0 * np.sqrt(FH * FW / C) / s[None, :]),
            "kqv_b": bf(0.5 * np.random.standard_normal(OC))}


def reference(X, gn_w, gn_b, kqv_w, kqv_b):
    xg = f64(X).reshape(B, GROUPS, -1)
    mu = xg.mean(-1, keepdims=True)
    var = xg.var(-1, keepdims=True)
    xn = ((xg - mu) / np.sqrt(var + EPS)).reshape(B, C, P)
    xn = xn * f64(gn_w)[:, None] + f64(gn_b)[:, None]
    kqv = (mxq(f64(kqv_w), 1, "e4m3") @ mxq(xn, 1, "e4m3")) + f64(kqv_b)[:, None]
    return kqv.reshape(B, OC, RES, FH, RES, FW).mean(axis=(3, 5))

@@ -1,0 +1,282 @@
+from contextlib import ExitStack
+
+import concourse.masks as masks
+import concourse.mybir as mybir
+
+F32 = mybir.dt.float32
+BF16 = mybir.dt.bfloat16
+U32 = mybir.dt.uint32
+U8 = mybir.dt.uint8
+FP8X4 = mybir.dt.float8_e4m3fn_x4
+ALU = mybir.AluOpType
+ACT = mybir.ActivationFunctionType
+AXIS = mybir.AxisListType
+
+P = 128
+PACK = 4
+BATCH = 4
+CHANNELS = P * PACK
+OUT_CH = 256
+M_TILES = OUT_CH // P
+SIDE = 64
+PIXELS = SIDE * SIDE
+POOL = 4
+CELLS = (SIDE // POOL) * (SIDE // POOL)
+ROW_CLASS = POOL * CELLS
+GROUP_SIZE = PACK * PIXELS
+EPS = 1e-5
+PIVOT_PIXELS = 1024
+X_SLOTS = 10
+SCALAR_CLASSES = 1
+LATE_SCALAR_CLASSES = 2
+LATE_IMAGES = 2
+
+FLOPS = 2 * BATCH * OUT_CH * CHANNELS * PIXELS
+
+
+def tile_multihead_attn_pa_t_kernel(tc, X, gn_w, gn_b, kqv_w, kqv_b, out):
+    nc = tc.nc
+    with ExitStack() as ctx:
+        const = ctx.enter_context(tc.tile_pool(name="const", bufs=1))
+        x_pool = ctx.enter_context(tc.tile_pool(name="x", bufs=X_SLOTS))
+        y_pool = ctx.enter_context(tc.tile_pool(name="y", bufs=2))
+        v_pool = ctx.enter_context(tc.tile_pool(name="v_out", bufs=3))
+        g_s_pool = ctx.enter_context(tc.tile_pool(name="g_s", bufs=2))
+        unread_s_pool = ctx.enter_context(tc.tile_pool(name="unread_s", bufs=2))
+        q_pool = ctx.enter_context(tc.tile_pool(name="q", bufs=3))
+        stat = ctx.enter_context(tc.tile_pool(name="stat", bufs=BATCH))
+        res_pool = ctx.enter_context(tc.tile_pool(name="res", bufs=2))
+        psum_w = ctx.enter_context(tc.psum_pool(name="psum_w", bufs=1))
+        psum = ctx.enter_context(tc.psum_pool(name="psum", bufs=2))
+        ctx.enter_context(tc.manual_schedule())
+
+        w_rows = const.tile([P, M_TILES * CHANNELS], BF16)
+        nc.scalar.dma_start(
+            out=w_rows[:].rearrange("o (m c) -> o m c", m=M_TILES),
+            in_=kqv_w.rearrange("(m o) c -> o m c", o=P),
+        )
+        gain_bf = const.tile([P, PACK], BF16)
+        nc.scalar.dma_start(out=gain_bf[:], in_=gn_w.rearrange("(p j) -> p j", j=PACK))
+        shift_bf = const.tile([P, PACK], BF16)
+        nc.scalar.dma_start(out=shift_bf[:], in_=gn_b.rearrange("(p j) -> p j", j=PACK))
+        bias_bf = const.tile([P, M_TILES], BF16)
+        with nc.allow_non_contiguous_dma(reason="256 bias values, one output channel a partition"):
+            nc.scalar.dma_start(out=bias_bf[:], in_=kqv_b.rearrange("(m o) -> o m", o=P))
+
+        x_chunk = {}
+
+        def load_chunks(first, count):
+            for k in range(first, min(first + count, BATCH * PACK)):
+                b, j = divmod(k, PACK)
+                pixels = X[b].rearrange("(p j) h w -> p j (h w)", j=PACK)[:, j, :]
+                x_bj = x_pool.tile([P, PIXELS], BF16, name="x_bj")
+                if j == 0:
+                    nc.sync.dma_start(out=x_bj[:, :PIVOT_PIXELS], in_=pixels[:, :PIVOT_PIXELS])
+                    nc.sync.dma_start(out=x_bj[:, PIVOT_PIXELS:], in_=pixels[:, PIVOT_PIXELS:])
+                else:
+                    nc.sync.dma_start(out=x_bj[:], in_=pixels)
+                x_chunk[(b, j)] = x_bj
+
+        load_chunks(0, X_SLOTS)
+
+        one = const.tile([P, 1], F32)
+        nc.vector.memset(one[:], 1.0)
+        table_warm = const.tile([P, 1], F32)
+        nc.scalar.activation(out=table_warm[:], in_=one[:], func=ACT.Sqrt)
+
+        sum_x = {}
+        sum_sq = {}
+        neg_pivot = {}
+
+        def sums(b):
+            sum_x[b] = stat.tile([P, PACK + 1], F32, name="sum_x")
+            neg_pivot[b] = stat.tile([P, 1], F32, name="neg_pivot")
+            sum_sq[b] = stat.tile([P, PACK], F32, name="sum_sq")
+            for j in range(PACK):
+                x_bj = x_chunk[(b, j)]
+                unread_v = v_pool.tile([P, PIXELS], BF16, name="unread_v", tag="v_out", align_bytes=64)
+                if j == 0:
+                    nc.vector.tensor_scalar(
+                        out=unread_v[:, :PIVOT_PIXELS], in0=x_bj[:, :PIVOT_PIXELS], scalar1=1.0,
+                        scalar2=None, op0=ALU.mult, op1=ALU.add, accum_out=sum_x[b][:, 0:1],
+                    )
+                    nc.vector.tensor_scalar(
+                        out=neg_pivot[b][:], in0=sum_x[b][:, 0:1], scalar1=-1.0 / PIVOT_PIXELS,
+                        scalar2=None, op0=ALU.mult,
+                    )
+                    nc.vector.tensor_scalar(
+                        out=unread_v[:, PIVOT_PIXELS:], in0=x_bj[:, PIVOT_PIXELS:], scalar1=1.0,
+                        scalar2=None, op0=ALU.mult, op1=ALU.add, accum_out=sum_x[b][:, 1:2],
+                    )
+                else:
+                    nc.vector.tensor_scalar(
+                        out=unread_v[:], in0=x_bj[:], scalar1=1.0, scalar2=None,
+                        op0=ALU.mult, op1=ALU.add, accum_out=sum_x[b][:, j + 1 : j + 2],
+                    )
+                unread_s = unread_s_pool.tile([P, PIXELS], BF16, name="unread_s")
+                nc.scalar.activation(
+                    out=unread_s[:], in_=x_bj[:], func=ACT.Square, bias=neg_pivot[b][:, 0:1],
+                    scale=1.0, accum_out=sum_sq[b][:, j : j + 1],
+                )
+
+        sums(0)
+
+        eps_share = const.tile([P, 1], F32)
+        nc.vector.memset(eps_share[:], EPS / PACK)
+        gain = const.tile([P, PACK], F32)
+        nc.vector.tensor_copy(out=gain[:], in_=gain_bf[:])
+        neg_gain_over_n = const.tile([P, PACK], F32)
+        nc.vector.tensor_scalar(
+            out=neg_gain_over_n[:], in0=gain_bf[:], scalar1=-1.0 / GROUP_SIZE, scalar2=None,
+            op0=ALU.mult,
+        )
+        shift = const.tile([P, PACK], F32)
+        nc.vector.tensor_copy(out=shift[:], in_=shift_bf[:])
+        bias = const.tile([P, M_TILES], F32)
+        nc.vector.tensor_copy(out=bias[:], in_=bias_bf[:])
+
+        identity = const.tile([P, P], F32)
+        masks.make_identity(nc, identity[:])
+        w_words = w_rows[:].bitcast(F32).rearrange("o (m p u) -> o m u p", m=M_TILES, u=2)
+        w_t = psum_w.tile([P, 2, OUT_CH], F32)
+        for m in range(M_TILES):
+            for u in range(2):
+                nc.tensor.transpose(w_t[:, u, m * P : (m + 1) * P], w_words[:, m, u, :], identity[:])
+        w_grouped = const.tile([P, OUT_CH * PACK], BF16, align_bytes=64)
+        nc.vector.tensor_copy(
+            out=w_grouped[:].bitcast(F32).rearrange("p (o u) -> p o u", u=2),
+            in_=w_t[:].rearrange("p u o -> p o u"),
+        )
+        w_codes = const.tile([P, OUT_CH], U32, align_bytes=64)
+        w_scales = const.tile([P, OUT_CH], U8, align_bytes=64)
+        nc.vector.quantize_mx(out=w_codes[:].bitcast(FP8X4), scales=w_scales[:], in_=w_grouped[:])
+
+        neg_mean_gain = {}
+        std = {}
+
+        def moments(b):
+            total_x = stat.tile([P, 1], F32, name="total_x")
+            nc.vector.reduce_sum(out=total_x[:], in_=sum_x[b][:], axis=AXIS.X)
+            neg_mean_gain[b] = stat.tile([P, PACK], F32, name="neg_mean_gain")
+            nc.vector.tensor_scalar(
+                out=neg_mean_gain[b][:], in0=neg_gain_over_n[:], scalar1=total_x[:, 0:1],
+                scalar2=None, op0=ALU.mult,
+            )
+            offset_sq = stat.tile([P, 1], F32, name="offset_sq")
+            nc.scalar.activation(
+                out=offset_sq[:], in_=total_x[:], func=ACT.Square, bias=neg_pivot[b][:, 0:1],
+                scale=1.0 / GROUP_SIZE,
+            )
+            sq_share = stat.tile([P, PACK], F32, name="sq_share")
+            mean_sq_eps = stat.tile([P, 1], F32, name="mean_sq_eps")
+            nc.scalar.activation(
+                out=sq_share[:], in_=sum_sq[b][:], func=ACT.Identity, bias=eps_share[:, 0:1],
+                scale=1.0 / GROUP_SIZE, accum_out=mean_sq_eps[:],
+            )
+            std[b] = stat.tile([P, 1], F32, name="std")
+            nc.scalar.activation(
+                out=std[b][:], in_=offset_sq[:], func=ACT.Sqrt, bias=mean_sq_eps[:, 0:1], scale=-1.0
+            )
+
+        def normalise(b):
+            rstd = stat.tile([P, 1], F32, name="rstd")
+            nc.vector.reciprocal(out=rstd[:], in_=std[b][:])
+            a = stat.tile([P, PACK], F32, name="a")
+            nc.vector.tensor_scalar(
+                out=a[:], in0=gain[:], scalar1=rstd[:, 0:1], scalar2=None, op0=ALU.mult
+            )
+            c = stat.tile([P, PACK], F32, name="c")
+            nc.vector.scalar_tensor_tensor(
+                out=c[:], in0=neg_mean_gain[b][:], scalar=rstd[:, 0:1], in1=shift[:],
+                op0=ALU.mult, op1=ALU.add,
+            )
+            y = y_pool.tile([P, POOL, PACK, ROW_CLASS], BF16, name="y")
+            for j in range(PACK):
+                nc.vector.tensor_scalar(
+                    out=y[:, :, j, :].rearrange("p th (i w) -> p th i w", w=SIDE),
+                    in0=x_chunk[(b, j)][:].rearrange("p (i th w) -> p th i w", th=POOL, w=SIDE),
+                    scalar1=a[:, j : j + 1], scalar2=c[:, j : j + 1], op0=ALU.mult, op1=ALU.add,
+                )
+            load_chunks(X_SLOTS + PACK * b, PACK)
+            return y
+
+        def regroup(copy, g, y, th):
+            copy(
+                out=g[:].rearrange("p (tw cell j) -> p cell j tw", tw=POOL, j=PACK),
+                in_=y[:, th, :, :].rearrange("p j (cell tw) -> p cell j tw", tw=POOL),
+            )
+            return g
+
+        def regroup_on_scalar(y, th):
+            g_s = g_s_pool.tile([P, PIXELS], BF16, name="g_s", align_bytes=64)
+            return regroup(nc.scalar.copy, g_s, y, th)
+
+        def regroup_on_vector(y, th):
+            g_v = v_pool.tile([P, PIXELS], BF16, name="g_v", tag="v_out", align_bytes=64)
+            return regroup(nc.vector.tensor_copy, g_v, y, th)
+
+        def quantise_and_multiply(g, acc, th):
+            codes = q_pool.tile([P, POOL * CELLS], U32, name="codes", align_bytes=64)
+            scales = q_pool.tile([P, POOL * CELLS], U8, name="scales", align_bytes=64)
+            nc.vector.quantize_mx(out=codes[:].bitcast(FP8X4), scales=scales[:], in_=g[:])
+            for m in range(M_TILES):
+                for tw in range(POOL):
+                    plane = slice(tw * CELLS, (tw + 1) * CELLS)
+                    nc.tensor.matmul_mx(
+                        out=acc[m][:],
+                        lhsT=w_codes[:, m * P : (m + 1) * P].bitcast(FP8X4),
+                        lhsT_scale=w_scales[:, m * P : (m + 1) * P],
+                        rhs=codes[:, plane].bitcast(FP8X4),
+                        rhs_scale=scales[:, plane],
+                        start=(th == 0 and tw == 0),
+                        stop=(th == POOL - 1 and tw == POOL - 1),
+                    )
+
+        def leave_on_scalar(b, acc):
+            res0 = res_pool.tile([P, CELLS], F32, name="res0")
+            nc.scalar.activation(
+                out=res0[:], in_=acc[0][:], func=ACT.Identity, bias=bias[:, 0:1],
+                scale=1.0 / (POOL * POOL),
+            )
+            nc.scalar.dma_start(out=out[b, 0:P].rearrange("o i jj -> o (i jj)"), in_=res0[:])
+
+        def leave_on_vector(b, acc):
+            res1 = res_pool.tile([P, CELLS], F32, name="res1")
+            nc.vector.tensor_scalar(
+                out=res1[:], in0=acc[1][:], scalar1=1.0 / (POOL * POOL), scalar2=bias[:, 1:2],
+                op0=ALU.mult, op1=ALU.add,
+            )
+            nc.sync.dma_start(out=out[b, P:OUT_CH].rearrange("o i jj -> o (i jj)"), in_=res1[:])
+
+        moments(0)
+        sums(1)
+        moments(1)
+        y_next = normalise(0)
+        acc_done = None
+        for b in range(BATCH):
+            y = y_next
+            n_scalar = LATE_SCALAR_CLASSES if b >= BATCH - LATE_IMAGES else SCALAR_CLASSES
+            first_scalar = POOL - n_scalar
+            g = {}
+            g[first_scalar] = regroup_on_scalar(y, first_scalar)
+            if b > 0:
+                leave_on_scalar(b - 1, acc_done)
+            if b + 2 < BATCH:
+                sums(b + 2)
+                moments(b + 2)
+            for th in range(first_scalar + 1, POOL):
+                g[th] = regroup_on_scalar(y, th)
+            acc = [psum.tile([P, CELLS], F32, name="acc%d" % m) for m in range(M_TILES)]
+            for th in range(first_scalar):
+                g[th] = regroup_on_vector(y, th)
+                if th == 0 and b > 0:
+                    leave_on_vector(b - 1, acc_done)
+                if th > 0:
+                    quantise_and_multiply(g[th - 1], acc, th - 1)
+                if th == 1 and b + 1 < BATCH:
+                    y_next = normalise(b + 1)
+            for th in range(first_scalar - 1, POOL):
+                quantise_and_multiply(g[th], acc, th)
+            acc_done = acc
+        leave_on_scalar(BATCH - 1, acc_done)
+        leave_on_vector(BATCH - 1, acc_done)

@@ -26,10 +26,14 @@ ROW_CLASS = POOL * CELLS
 GROUP_SIZE = PACK * PIXELS
 EPS = 1e-5
 PIVOT_PIXELS = 1024
-X_SLOTS = 10
-SCALAR_CLASSES = 1
-LATE_SCALAR_CLASSES = 2
-LATE_IMAGES = 2
+X_SLOTS = 8
+PE_SUM_FROM = 2
+SLABS = 8
+RUN = 2048
+PARTS_OF_GROUP = 8
+CLASSES = 16
+SLABS_PER_LOAD = 2
+SCALAR_CLASSES = (0, 0, 1, 2)
 
 FLOPS = 2 * BATCH * OUT_CH * CHANNELS * PIXELS
 
@@ -39,6 +43,9 @@ def tile_multihead_attn_pa_t_kernel(tc, X, gn_w, gn_b, kqv_w, kqv_b, out):
     with ExitStack() as ctx:
         const = ctx.enter_context(tc.tile_pool(name="const", bufs=1))
         x_pool = ctx.enter_context(tc.tile_pool(name="x", bufs=X_SLOTS))
+        x2_pool = ctx.enter_context(tc.tile_pool(name="x2", bufs=2))
+        junk_pool = ctx.enter_context(tc.tile_pool(name="junk", bufs=1))
+        part_pool = ctx.enter_context(tc.tile_pool(name="part", bufs=2))
         y_pool = ctx.enter_context(tc.tile_pool(name="y", bufs=2))
         v_pool = ctx.enter_context(tc.tile_pool(name="v_out", bufs=3))
         g_s_pool = ctx.enter_context(tc.tile_pool(name="g_s", bufs=2))
@@ -48,6 +55,7 @@ def tile_multihead_attn_pa_t_kernel(tc, X, gn_w, gn_b, kqv_w, kqv_b, out):
         res_pool = ctx.enter_context(tc.tile_pool(name="res", bufs=2))
         psum_w = ctx.enter_context(tc.psum_pool(name="psum_w", bufs=1))
         psum = ctx.enter_context(tc.psum_pool(name="psum", bufs=2))
+        psum_s = ctx.enter_context(tc.psum_pool(name="psum_s", bufs=2))
         ctx.enter_context(tc.manual_schedule())
 
         w_rows = const.tile([P, M_TILES * CHANNELS], BF16)
@@ -79,6 +87,24 @@ def tile_multihead_attn_pa_t_kernel(tc, X, gn_w, gn_b, kqv_w, kqv_b, out):
 
         load_chunks(0, X_SLOTS)
 
+        LOADS = SLABS // SLABS_PER_LOAD
+        x2_list = [(b, h) for b in range(PE_SUM_FROM, BATCH) for h in range(LOADS)]
+        x2_tile = {}
+
+        def load_x2(i):
+            if i >= len(x2_list):
+                return
+            b, h = x2_list[i]
+            slabs = X[b].rearrange("c h w -> (c h w)").rearrange("(s k e) -> k s e", s=SLABS, k=P)
+            x2 = x2_pool.tile([P, SLABS_PER_LOAD, RUN], BF16, name="x2")
+            nc.sync.dma_start(
+                out=x2[:], in_=slabs[:, h * SLABS_PER_LOAD : (h + 1) * SLABS_PER_LOAD, :]
+            )
+            x2_tile[i] = x2
+
+        load_x2(0)
+        load_x2(1)
+
         one = const.tile([P, 1], F32)
         nc.vector.memset(one[:], 1.0)
         table_warm = const.tile([P, 1], F32)
@@ -87,6 +113,56 @@ def tile_multihead_attn_pa_t_kernel(tc, X, gn_w, gn_b, kqv_w, kqv_b, out):
         sum_x = {}
         sum_sq = {}
         neg_pivot = {}
+
+        def pivot(b):
+            sum_x[b] = stat.tile([P, 1], F32, name="sum_pivot")
+            neg_pivot[b] = stat.tile([P, 1], F32, name="neg_pivot")
+            junk = junk_pool.tile([P, PIVOT_PIXELS], BF16, name="junk")
+            nc.vector.tensor_scalar(
+                out=junk[:], in0=x_chunk[(b, 0)][:, :PIVOT_PIXELS], scalar1=1.0,
+                scalar2=None, op0=ALU.mult, op1=ALU.add, accum_out=sum_x[b][:, 0:1],
+            )
+            nc.vector.tensor_scalar(
+                out=neg_pivot[b][:], in0=sum_x[b][:, 0:1], scalar1=-1.0 / PIVOT_PIXELS,
+                scalar2=None, op0=ALU.mult,
+            )
+
+        def squares(b):
+            sum_sq[b] = stat.tile([P, PACK], F32, name="sum_sq")
+            for j in range(PACK):
+                unread_s = unread_s_pool.tile([P, PIXELS], BF16, name="unread_s")
+                nc.scalar.activation(
+                    out=unread_s[:], in_=x_chunk[(b, j)][:], func=ACT.Square,
+                    bias=neg_pivot[b][:, 0:1], scale=1.0, accum_out=sum_sq[b][:, j : j + 1],
+                )
+
+        part_sums = {}
+
+        def sum_on_tensor(i):
+            b, h = x2_list[i]
+            if h == 0:
+                part_sums[b] = psum_s.tile([P, 512], F32, name="part_sums")
+            for s in range(SLABS_PER_LOAD):
+                first = (h * SLABS_PER_LOAD + s) * CLASSES
+                for c in range(RUN // P):
+                    nc.tensor.matmul(
+                        out=part_sums[b][:, first : first + CLASSES],
+                        lhsT=x2_tile[i][:, s, c * P : (c + 1) * P],
+                        rhs=class_mask[:],
+                        start=(c == 0),
+                        stop=(c == RUN // P - 1),
+                    )
+
+        total_x = {}
+
+        def finish_sum_on_tensor(b):
+            part = part_pool.tile([P, P], F32, name="part")
+            nc.vector.tensor_copy(out=part[:], in_=part_sums[b][:, :P])
+            nc.tensor.matmul(
+                out=part_sums[b][:, P : P + 1], lhsT=part[:], rhs=one[:], start=True, stop=True
+            )
+            total_x[b] = stat.tile([P, 1], F32, name="total_x")
+            nc.vector.tensor_copy(out=total_x[b][:], in_=part_sums[b][:, P : P + 1])
 
         def sums(b):
             sum_x[b] = stat.tile([P, PACK + 1], F32, name="sum_x")
@@ -137,6 +213,16 @@ def tile_multihead_attn_pa_t_kernel(tc, X, gn_w, gn_b, kqv_w, kqv_b, out):
 
         identity = const.tile([P, P], F32)
         masks.make_identity(nc, identity[:])
+        class_mask = const.tile([P, CLASSES], BF16)
+        nc.gpsimd.memset(class_mask[:], 1.0)
+        nc.gpsimd.affine_select(
+            out=class_mask[:], in_=class_mask[:], compare_op=ALU.is_ge, fill=0.0, base=0,
+            pattern=[[-PARTS_OF_GROUP, CLASSES]], channel_multiplier=1,
+        )
+        nc.gpsimd.affine_select(
+            out=class_mask[:], in_=class_mask[:], compare_op=ALU.is_ge, fill=0.0,
+            base=PARTS_OF_GROUP - 1, pattern=[[PARTS_OF_GROUP, CLASSES]], channel_multiplier=-1,
+        )
         w_words = w_rows[:].bitcast(F32).rearrange("o (m p u) -> o m u p", m=M_TILES, u=2)
         w_t = psum_w.tile([P, 2, OUT_CH], F32)
         for m in range(M_TILES):
@@ -155,16 +241,17 @@ def tile_multihead_attn_pa_t_kernel(tc, X, gn_w, gn_b, kqv_w, kqv_b, out):
         std = {}
 
         def moments(b):
-            total_x = stat.tile([P, 1], F32, name="total_x")
-            nc.vector.reduce_sum(out=total_x[:], in_=sum_x[b][:], axis=AXIS.X)
+            if b < PE_SUM_FROM:
+                total_x[b] = stat.tile([P, 1], F32, name="total_x")
+                nc.vector.reduce_sum(out=total_x[b][:], in_=sum_x[b][:], axis=AXIS.X)
             neg_mean_gain[b] = stat.tile([P, PACK], F32, name="neg_mean_gain")
             nc.vector.tensor_scalar(
-                out=neg_mean_gain[b][:], in0=neg_gain_over_n[:], scalar1=total_x[:, 0:1],
+                out=neg_mean_gain[b][:], in0=neg_gain_over_n[:], scalar1=total_x[b][:, 0:1],
                 scalar2=None, op0=ALU.mult,
             )
             offset_sq = stat.tile([P, 1], F32, name="offset_sq")
             nc.scalar.activation(
-                out=offset_sq[:], in_=total_x[:], func=ACT.Square, bias=neg_pivot[b][:, 0:1],
+                out=offset_sq[:], in_=total_x[b][:], func=ACT.Square, bias=neg_pivot[b][:, 0:1],
                 scale=1.0 / GROUP_SIZE,
             )
             sq_share = stat.tile([P, PACK], F32, name="sq_share")
@@ -255,28 +342,34 @@ def tile_multihead_attn_pa_t_kernel(tc, X, gn_w, gn_b, kqv_w, kqv_b, out):
         acc_done = None
         for b in range(BATCH):
             y = y_next
-            n_scalar = LATE_SCALAR_CLASSES if b >= BATCH - LATE_IMAGES else SCALAR_CLASSES
-            first_scalar = POOL - n_scalar
+            first_scalar = POOL - SCALAR_CLASSES[b]
             g = {}
-            g[first_scalar] = regroup_on_scalar(y, first_scalar)
+            if first_scalar < POOL:
+                g[first_scalar] = regroup_on_scalar(y, first_scalar)
             if b > 0:
                 leave_on_scalar(b - 1, acc_done)
-            if b + 2 < BATCH:
-                sums(b + 2)
-                moments(b + 2)
             for th in range(first_scalar + 1, POOL):
                 g[th] = regroup_on_scalar(y, th)
             acc = [psum.tile([P, CELLS], F32, name="acc%d" % m) for m in range(M_TILES)]
-            for th in range(first_scalar):
-                g[th] = regroup_on_vector(y, th)
+            for th in range(POOL):
+                if th < first_scalar:
+                    g[th] = regroup_on_vector(y, th)
                 if th == 0 and b > 0:
                     leave_on_vector(b - 1, acc_done)
+                if b + 2 < BATCH:
+                    sum_on_tensor(POOL * b + th)
+                    load_x2(POOL * b + th + 2)
                 if th > 0:
                     quantise_and_multiply(g[th - 1], acc, th - 1)
-                if th == 1 and b + 1 < BATCH:
-                    y_next = normalise(b + 1)
-            for th in range(first_scalar - 1, POOL):
-                quantise_and_multiply(g[th], acc, th)
+                if th == 1 and b + 2 < BATCH:
+                    pivot(b + 2)
+                    squares(b + 2)
+            if b + 1 < BATCH:
+                y_next = normalise(b + 1)
+            quantise_and_multiply(g[POOL - 1], acc, POOL - 1)
+            if b + 2 < BATCH:
+                finish_sum_on_tensor(b + 2)
+                moments(b + 2)
             acc_done = acc
         leave_on_scalar(BATCH - 1, acc_done)
         leave_on_vector(BATCH - 1, acc_done)

@@ -27,13 +27,16 @@ GROUP_SIZE = PACK * PIXELS
 EPS = 1e-5
 PIVOT_PIXELS = 1024
 X_SLOTS = 8
-PE_SUM_FROM = 2
+PE_SUM_FROM = 1
 SLABS = 8
 RUN = 2048
 PARTS_OF_GROUP = 8
 CLASSES = 16
 SLABS_PER_LOAD = 2
 SCALAR_CLASSES = (0, 0, 1, 2)
+HEAD_SPLIT = 3584
+BN_WIDTH = 512
+BN_PIECES = (2 * PIXELS - HEAD_SPLIT) // BN_WIDTH
 
 FLOPS = 2 * BATCH * OUT_CH * CHANNELS * PIXELS
 
@@ -43,13 +46,13 @@ def tile_multihead_attn_pa_t_kernel(tc, X, gn_w, gn_b, kqv_w, kqv_b, out):
     with ExitStack() as ctx:
         const = ctx.enter_context(tc.tile_pool(name="const", bufs=1))
         x_pool = ctx.enter_context(tc.tile_pool(name="x", bufs=X_SLOTS))
-        x2_pool = ctx.enter_context(tc.tile_pool(name="x2", bufs=2))
+        x2_pool = ctx.enter_context(tc.tile_pool(name="x2", bufs=4))
         junk_pool = ctx.enter_context(tc.tile_pool(name="junk", bufs=1))
         part_pool = ctx.enter_context(tc.tile_pool(name="part", bufs=2))
         y_pool = ctx.enter_context(tc.tile_pool(name="y", bufs=2))
-        v_pool = ctx.enter_context(tc.tile_pool(name="v_out", bufs=3))
+        v_pool = ctx.enter_context(tc.tile_pool(name="v_out", bufs=2))
         g_s_pool = ctx.enter_context(tc.tile_pool(name="g_s", bufs=2))
-        unread_s_pool = ctx.enter_context(tc.tile_pool(name="unread_s", bufs=2))
+        unread_s_pool = ctx.enter_context(tc.tile_pool(name="unread_s", bufs=1))
         q_pool = ctx.enter_context(tc.tile_pool(name="q", bufs=3))
         stat = ctx.enter_context(tc.tile_pool(name="stat", bufs=BATCH))
         res_pool = ctx.enter_context(tc.tile_pool(name="res", bufs=2))
@@ -85,56 +88,162 @@ def tile_multihead_attn_pa_t_kernel(tc, X, gn_w, gn_b, kqv_w, kqv_b, out):
                     nc.sync.dma_start(out=x_bj[:], in_=pixels)
                 x_chunk[(b, j)] = x_bj
 
-        load_chunks(0, X_SLOTS)
-
         LOADS = SLABS // SLABS_PER_LOAD
         x2_list = [(b, h) for b in range(PE_SUM_FROM, BATCH) for h in range(LOADS)]
         x2_tile = {}
 
-        def load_x2(i):
-            if i >= len(x2_list):
-                return
-            b, h = x2_list[i]
-            slabs = X[b].rearrange("c h w -> (c h w)").rearrange("(s k e) -> k s e", s=SLABS, k=P)
-            x2 = x2_pool.tile([P, SLABS_PER_LOAD, RUN], BF16, name="x2")
-            nc.sync.dma_start(
-                out=x2[:], in_=slabs[:, h * SLABS_PER_LOAD : (h + 1) * SLABS_PER_LOAD, :]
-            )
-            x2_tile[i] = x2
+        def load_x2(first, count):
+            for i in range(first, min(first + count, len(x2_list))):
+                b, h = x2_list[i]
+                slabs = X[b].rearrange("c h w -> (c h w)").rearrange(
+                    "(s k e) -> k s e", s=SLABS, k=P
+                )
+                x2 = x2_pool.tile([P, SLABS_PER_LOAD, RUN], BF16, name="x2")
+                nc.sync.dma_start(
+                    out=x2[:], in_=slabs[:, h * SLABS_PER_LOAD : (h + 1) * SLABS_PER_LOAD, :]
+                )
+                x2_tile[i] = x2
 
-        load_x2(0)
-        load_x2(1)
+        def load_image(b):
+            load_chunks(PACK * b, 1)
+            load_x2(LOADS * (b - PE_SUM_FROM), 2)
+            load_chunks(PACK * b + 1, 1)
+            load_x2(LOADS * (b - PE_SUM_FROM) + 2, 2)
+            load_chunks(PACK * b + 2, 2)
+
+        load_chunks(0, PACK)
+        load_image(1)
 
         one = const.tile([P, 1], F32)
         nc.vector.memset(one[:], 1.0)
         table_warm = const.tile([P, 1], F32)
         nc.scalar.activation(out=table_warm[:], in_=one[:], func=ACT.Sqrt)
+        eps_share = const.tile([P, 1], F32)
+        nc.vector.memset(eps_share[:], EPS / PACK)
 
-        sum_x = {}
+        class_mask = const.tile([P, CLASSES], BF16)
+        nc.gpsimd.memset(class_mask[:], 1.0)
+        nc.gpsimd.affine_select(
+            out=class_mask[:], in_=class_mask[:], compare_op=ALU.is_ge, fill=0.0, base=0,
+            pattern=[[-PARTS_OF_GROUP, CLASSES]], channel_multiplier=1,
+        )
+        nc.gpsimd.affine_select(
+            out=class_mask[:], in_=class_mask[:], compare_op=ALU.is_ge, fill=0.0,
+            base=PARTS_OF_GROUP - 1, pattern=[[PARTS_OF_GROUP, CLASSES]], channel_multiplier=-1,
+        )
+        identity = const.tile([P, P], F32)
+        masks.make_identity(nc, identity[:])
+
+        w_words = w_rows[:].bitcast(F32).rearrange("o (m p u) -> o m u p", m=M_TILES, u=2)
+        w_t = psum_w.tile([P, 2, OUT_CH], F32)
+        for m in range(M_TILES):
+            for u in range(2):
+                nc.tensor.transpose(w_t[:, u, m * P : (m + 1) * P], w_words[:, m, u, :], identity[:])
+        w_grouped = const.tile([P, OUT_CH * PACK], BF16, align_bytes=64)
+        w_codes = const.tile([P, OUT_CH], U32, align_bytes=64)
+        w_scales = const.tile([P, OUT_CH], U8, align_bytes=64)
+
+        def quantise_weights():
+            nc.vector.tensor_copy(
+                out=w_grouped[:].bitcast(F32).rearrange("p (o u) -> p o u", u=2),
+                in_=w_t[:].rearrange("p u o -> p o u"),
+            )
+            nc.vector.quantize_mx(
+                out=w_codes[:].bitcast(FP8X4), scales=w_scales[:], in_=w_grouped[:]
+            )
+
         sum_sq = {}
         neg_pivot = {}
+        total_x = {}
 
-        def pivot(b):
-            sum_x[b] = stat.tile([P, 1], F32, name="sum_pivot")
+        def sum_on_vector(x_bj, lo, hi, accum):
+            unread_v = v_pool.tile([P, PIXELS], BF16, name="unread_v", tag="v_out", align_bytes=64)
+            nc.vector.tensor_scalar(
+                out=unread_v[:, lo:hi], in0=x_bj[:, lo:hi], scalar1=1.0, scalar2=None,
+                op0=ALU.mult, op1=ALU.add, accum_out=accum,
+            )
+
+        def pivot(b, sum_pivot):
             neg_pivot[b] = stat.tile([P, 1], F32, name="neg_pivot")
             junk = junk_pool.tile([P, PIVOT_PIXELS], BF16, name="junk")
             nc.vector.tensor_scalar(
                 out=junk[:], in0=x_chunk[(b, 0)][:, :PIVOT_PIXELS], scalar1=1.0,
-                scalar2=None, op0=ALU.mult, op1=ALU.add, accum_out=sum_x[b][:, 0:1],
+                scalar2=None, op0=ALU.mult, op1=ALU.add, accum_out=sum_pivot,
             )
             nc.vector.tensor_scalar(
-                out=neg_pivot[b][:], in0=sum_x[b][:, 0:1], scalar1=-1.0 / PIVOT_PIXELS,
+                out=neg_pivot[b][:], in0=sum_pivot, scalar1=-1.0 / PIVOT_PIXELS,
                 scalar2=None, op0=ALU.mult,
+            )
+
+        def later_pivot(b):
+            sum_pivot = stat.tile([P, 1], F32, name="sum_pivot")
+            pivot(b, sum_pivot[:])
+
+        def square_on_scalar(b, j, width):
+            unread_s = unread_s_pool.tile([P, PIXELS], BF16, name="unread_s")
+            nc.scalar.activation(
+                out=unread_s[:, :width], in_=x_chunk[(b, j)][:, :width], func=ACT.Square,
+                bias=neg_pivot[b][:, 0:1], scale=1.0, accum_out=sum_sq[b][:, j : j + 1],
             )
 
         def squares(b):
             sum_sq[b] = stat.tile([P, PACK], F32, name="sum_sq")
             for j in range(PACK):
-                unread_s = unread_s_pool.tile([P, PIXELS], BF16, name="unread_s")
-                nc.scalar.activation(
-                    out=unread_s[:], in_=x_chunk[(b, j)][:], func=ACT.Square,
-                    bias=neg_pivot[b][:, 0:1], scale=1.0, accum_out=sum_sq[b][:, j : j + 1],
-                )
+                square_on_scalar(b, j, PIXELS)
+
+        sum_x0 = const.tile([P, PACK + 1], F32)
+        sum_sq[0] = stat.tile([P, PACK], F32, name="sum_sq")
+        pivot(0, sum_x0[:, 0:1])
+        sum_on_vector(x_chunk[(0, 0)], PIVOT_PIXELS, PIXELS, sum_x0[:, 1:2])
+        square_on_scalar(0, 0, PIXELS)
+        sum_on_vector(x_chunk[(0, 1)], 0, PIXELS, sum_x0[:, 2:3])
+        square_on_scalar(0, 1, PIXELS)
+
+        gain = const.tile([P, PACK], F32)
+        nc.vector.tensor_copy(out=gain[:], in_=gain_bf[:])
+        neg_gain_over_n = const.tile([P, PACK], F32)
+        nc.vector.tensor_scalar(
+            out=neg_gain_over_n[:], in0=gain_bf[:], scalar1=-1.0 / GROUP_SIZE, scalar2=None,
+            op0=ALU.mult,
+        )
+        shift = const.tile([P, PACK], F32)
+        nc.vector.tensor_copy(out=shift[:], in_=shift_bf[:])
+        bias = const.tile([P, M_TILES], F32)
+        nc.vector.tensor_copy(out=bias[:], in_=bias_bf[:])
+
+        sum_on_vector(x_chunk[(0, 2)], 0, HEAD_SPLIT, sum_x0[:, 3:4])
+        square_on_scalar(0, 2, HEAD_SPLIT)
+        bn_out = const.tile([P, BN_PIECES, 6], F32)
+        for i in range(BN_PIECES):
+            first = HEAD_SPLIT + i * BN_WIDTH
+            nc.vector.bn_stats(
+                out=bn_out[:, i, :],
+                in_=x_chunk[(0, 2 + first // PIXELS)][:, first % PIXELS : first % PIXELS + BN_WIDTH],
+            )
+            if i == BN_PIECES // 2:
+                later_pivot(1)
+        mean_var = const.tile([P, 2], F32)
+        nc.vector.bn_aggr(out=mean_var[:], in_=bn_out[:].rearrange("p i s -> p (i s)"))
+        nc.vector.tensor_scalar(
+            out=sum_x0[:, 4:5], in0=mean_var[:, 0:1], scalar1=float(BN_PIECES * BN_WIDTH),
+            scalar2=None, op0=ALU.mult,
+        )
+        off_pivot = const.tile([P, 1], F32)
+        nc.vector.tensor_scalar(
+            out=off_pivot[:], in0=mean_var[:, 0:1], scalar1=neg_pivot[0][:, 0:1], scalar2=None,
+            op0=ALU.add,
+        )
+        mean_sq_off = const.tile([P, 1], F32)
+        nc.vector.scalar_tensor_tensor(
+            out=mean_sq_off[:], in0=off_pivot[:], scalar=off_pivot[:, 0:1], in1=mean_var[:, 1:2],
+            op0=ALU.mult, op1=ALU.add,
+        )
+        nc.vector.tensor_scalar(
+            out=sum_sq[0][:, 3:4], in0=mean_sq_off[:], scalar1=float(BN_PIECES * BN_WIDTH),
+            scalar2=None, op0=ALU.mult,
+        )
+        total_x[0] = stat.tile([P, 1], F32, name="total_x")
+        nc.vector.reduce_sum(out=total_x[0][:], in_=sum_x0[:], axis=AXIS.X)
 
         part_sums = {}
 
@@ -153,97 +262,21 @@ def tile_multihead_attn_pa_t_kernel(tc, X, gn_w, gn_b, kqv_w, kqv_b, out):
                         stop=(c == RUN // P - 1),
                     )
 
-        total_x = {}
-
-        def finish_sum_on_tensor(b):
+        def gather_total(b):
             part = part_pool.tile([P, P], F32, name="part")
             nc.vector.tensor_copy(out=part[:], in_=part_sums[b][:, :P])
             nc.tensor.matmul(
                 out=part_sums[b][:, P : P + 1], lhsT=part[:], rhs=one[:], start=True, stop=True
             )
+
+        def read_total(b):
             total_x[b] = stat.tile([P, 1], F32, name="total_x")
             nc.vector.tensor_copy(out=total_x[b][:], in_=part_sums[b][:, P : P + 1])
-
-        def sums(b):
-            sum_x[b] = stat.tile([P, PACK + 1], F32, name="sum_x")
-            neg_pivot[b] = stat.tile([P, 1], F32, name="neg_pivot")
-            sum_sq[b] = stat.tile([P, PACK], F32, name="sum_sq")
-            for j in range(PACK):
-                x_bj = x_chunk[(b, j)]
-                unread_v = v_pool.tile([P, PIXELS], BF16, name="unread_v", tag="v_out", align_bytes=64)
-                if j == 0:
-                    nc.vector.tensor_scalar(
-                        out=unread_v[:, :PIVOT_PIXELS], in0=x_bj[:, :PIVOT_PIXELS], scalar1=1.0,
-                        scalar2=None, op0=ALU.mult, op1=ALU.add, accum_out=sum_x[b][:, 0:1],
-                    )
-                    nc.vector.tensor_scalar(
-                        out=neg_pivot[b][:], in0=sum_x[b][:, 0:1], scalar1=-1.0 / PIVOT_PIXELS,
-                        scalar2=None, op0=ALU.mult,
-                    )
-                    nc.vector.tensor_scalar(
-                        out=unread_v[:, PIVOT_PIXELS:], in0=x_bj[:, PIVOT_PIXELS:], scalar1=1.0,
-                        scalar2=None, op0=ALU.mult, op1=ALU.add, accum_out=sum_x[b][:, 1:2],
-                    )
-                else:
-                    nc.vector.tensor_scalar(
-                        out=unread_v[:], in0=x_bj[:], scalar1=1.0, scalar2=None,
-                        op0=ALU.mult, op1=ALU.add, accum_out=sum_x[b][:, j + 1 : j + 2],
-                    )
-                unread_s = unread_s_pool.tile([P, PIXELS], BF16, name="unread_s")
-                nc.scalar.activation(
-                    out=unread_s[:], in_=x_bj[:], func=ACT.Square, bias=neg_pivot[b][:, 0:1],
-                    scale=1.0, accum_out=sum_sq[b][:, j : j + 1],
-                )
-
-        sums(0)
-
-        eps_share = const.tile([P, 1], F32)
-        nc.vector.memset(eps_share[:], EPS / PACK)
-        gain = const.tile([P, PACK], F32)
-        nc.vector.tensor_copy(out=gain[:], in_=gain_bf[:])
-        neg_gain_over_n = const.tile([P, PACK], F32)
-        nc.vector.tensor_scalar(
-            out=neg_gain_over_n[:], in0=gain_bf[:], scalar1=-1.0 / GROUP_SIZE, scalar2=None,
-            op0=ALU.mult,
-        )
-        shift = const.tile([P, PACK], F32)
-        nc.vector.tensor_copy(out=shift[:], in_=shift_bf[:])
-        bias = const.tile([P, M_TILES], F32)
-        nc.vector.tensor_copy(out=bias[:], in_=bias_bf[:])
-
-        identity = const.tile([P, P], F32)
-        masks.make_identity(nc, identity[:])
-        class_mask = const.tile([P, CLASSES], BF16)
-        nc.gpsimd.memset(class_mask[:], 1.0)
-        nc.gpsimd.affine_select(
-            out=class_mask[:], in_=class_mask[:], compare_op=ALU.is_ge, fill=0.0, base=0,
-            pattern=[[-PARTS_OF_GROUP, CLASSES]], channel_multiplier=1,
-        )
-        nc.gpsimd.affine_select(
-            out=class_mask[:], in_=class_mask[:], compare_op=ALU.is_ge, fill=0.0,
-            base=PARTS_OF_GROUP - 1, pattern=[[PARTS_OF_GROUP, CLASSES]], channel_multiplier=-1,
-        )
-        w_words = w_rows[:].bitcast(F32).rearrange("o (m p u) -> o m u p", m=M_TILES, u=2)
-        w_t = psum_w.tile([P, 2, OUT_CH], F32)
-        for m in range(M_TILES):
-            for u in range(2):
-                nc.tensor.transpose(w_t[:, u, m * P : (m + 1) * P], w_words[:, m, u, :], identity[:])
-        w_grouped = const.tile([P, OUT_CH * PACK], BF16, align_bytes=64)
-        nc.vector.tensor_copy(
-            out=w_grouped[:].bitcast(F32).rearrange("p (o u) -> p o u", u=2),
-            in_=w_t[:].rearrange("p u o -> p o u"),
-        )
-        w_codes = const.tile([P, OUT_CH], U32, align_bytes=64)
-        w_scales = const.tile([P, OUT_CH], U8, align_bytes=64)
-        nc.vector.quantize_mx(out=w_codes[:].bitcast(FP8X4), scales=w_scales[:], in_=w_grouped[:])
 
         neg_mean_gain = {}
         std = {}
 
         def moments(b):
-            if b < PE_SUM_FROM:
-                total_x[b] = stat.tile([P, 1], F32, name="total_x")
-                nc.vector.reduce_sum(out=total_x[b][:], in_=sum_x[b][:], axis=AXIS.X)
             neg_mean_gain[b] = stat.tile([P, PACK], F32, name="neg_mean_gain")
             nc.vector.tensor_scalar(
                 out=neg_mean_gain[b][:], in0=neg_gain_over_n[:], scalar1=total_x[b][:, 0:1],
@@ -284,7 +317,8 @@ def tile_multihead_attn_pa_t_kernel(tc, X, gn_w, gn_b, kqv_w, kqv_b, out):
                     in0=x_chunk[(b, j)][:].rearrange("p (i th w) -> p th i w", th=POOL, w=SIDE),
                     scalar1=a[:, j : j + 1], scalar2=c[:, j : j + 1], op0=ALU.mult, op1=ALU.add,
                 )
-            load_chunks(X_SLOTS + PACK * b, PACK)
+            if b + 2 < BATCH:
+                load_image(b + 2)
             return y
 
         def regroup(copy, g, y, th):
@@ -336,40 +370,47 @@ def tile_multihead_attn_pa_t_kernel(tc, X, gn_w, gn_b, kqv_w, kqv_b, out):
             nc.sync.dma_start(out=out[b, P:OUT_CH].rearrange("o i jj -> o (i jj)"), in_=res1[:])
 
         moments(0)
-        sums(1)
-        moments(1)
+        squares(1)
+        for i in range(LOADS):
+            sum_on_tensor(i)
         y_next = normalise(0)
         acc_done = None
         for b in range(BATCH):
             y = y_next
             first_scalar = POOL - SCALAR_CLASSES[b]
             g = {}
-            if first_scalar < POOL:
-                g[first_scalar] = regroup_on_scalar(y, first_scalar)
+            if b == BATCH - 1:
+                for th in range(first_scalar, POOL):
+                    g[th] = regroup_on_scalar(y, th)
             if b > 0:
                 leave_on_scalar(b - 1, acc_done)
-            for th in range(first_scalar + 1, POOL):
-                g[th] = regroup_on_scalar(y, th)
             acc = [psum.tile([P, CELLS], F32, name="acc%d" % m) for m in range(M_TILES)]
             for th in range(POOL):
                 if th < first_scalar:
                     g[th] = regroup_on_vector(y, th)
+                if th == 0 and b == 0:
+                    quantise_weights()
+                    gather_total(1)
                 if th == 0 and b > 0:
                     leave_on_vector(b - 1, acc_done)
+                if th == 1 and b + 1 < BATCH:
+                    read_total(b + 1)
                 if b + 2 < BATCH:
-                    sum_on_tensor(POOL * b + th)
-                    load_x2(POOL * b + th + 2)
+                    sum_on_tensor(LOADS * (b + 1) + th)
+                if th == POOL - 1 and b + 1 < BATCH:
+                    moments(b + 1)
+                    if b + 2 < BATCH:
+                        squares(b + 2)
+                    for late in range(first_scalar, POOL):
+                        g[late] = regroup_on_scalar(y, late)
+                    y_next = normalise(b + 1)
                 if th > 0:
                     quantise_and_multiply(g[th - 1], acc, th - 1)
-                if th == 1 and b + 2 < BATCH:
-                    pivot(b + 2)
-                    squares(b + 2)
-            if b + 1 < BATCH:
-                y_next = normalise(b + 1)
+                if th == 2 and b + 2 < BATCH:
+                    later_pivot(b + 2)
             quantise_and_multiply(g[POOL - 1], acc, POOL - 1)
             if b + 2 < BATCH:
-                finish_sum_on_tensor(b + 2)
-                moments(b + 2)
+                gather_total(b + 2)
             acc_done = acc
         leave_on_scalar(BATCH - 1, acc_done)
         leave_on_vector(BATCH - 1, acc_done)

@@ -25,7 +25,7 @@ CELLS = (SIDE // POOL) * (SIDE // POOL)
 ROW_CLASS = POOL * CELLS
 GROUP_SIZE = PACK * PIXELS
 EPS = 1e-5
-PIVOT_PIXELS = 1024
+PIVOT_PIXELS = 256
 X_SLOTS = 8
 PE_SUM_FROM = 1
 SLABS = 8
@@ -33,10 +33,13 @@ RUN = 2048
 PARTS_OF_GROUP = 8
 CLASSES = 16
 SLABS_PER_LOAD = 2
+X2_SLOTS = 4
 SCALAR_CLASSES = (0, 0, 1, 2)
-HEAD_SPLIT = 3584
+HEAD_SCALAR = 2560
+HEAD_FOLD_3 = 1024
 BN_WIDTH = 512
-BN_PIECES = (2 * PIXELS - HEAD_SPLIT) // BN_WIDTH
+BN_PER_CHUNK = (PIXELS - HEAD_SCALAR) // BN_WIDTH
+BN_VALUES = PACK * BN_PER_CHUNK * BN_WIDTH
 
 FLOPS = 2 * BATCH * OUT_CH * CHANNELS * PIXELS
 
@@ -46,7 +49,7 @@ def tile_multihead_attn_pa_t_kernel(tc, X, gn_w, gn_b, kqv_w, kqv_b, out):
     with ExitStack() as ctx:
         const = ctx.enter_context(tc.tile_pool(name="const", bufs=1))
         x_pool = ctx.enter_context(tc.tile_pool(name="x", bufs=X_SLOTS))
-        x2_pool = ctx.enter_context(tc.tile_pool(name="x2", bufs=4))
+        x2_pool = ctx.enter_context(tc.tile_pool(name="x2", bufs=X2_SLOTS))
         junk_pool = ctx.enter_context(tc.tile_pool(name="junk", bufs=1))
         part_pool = ctx.enter_context(tc.tile_pool(name="part", bufs=2))
         y_pool = ctx.enter_context(tc.tile_pool(name="y", bufs=2))
@@ -104,22 +107,33 @@ def tile_multihead_attn_pa_t_kernel(tc, X, gn_w, gn_b, kqv_w, kqv_b, out):
                 )
                 x2_tile[i] = x2
 
-        def load_image(b):
-            load_chunks(PACK * b, 1)
-            load_x2(LOADS * (b - PE_SUM_FROM), 2)
-            load_chunks(PACK * b + 1, 1)
-            load_x2(LOADS * (b - PE_SUM_FROM) + 2, 2)
-            load_chunks(PACK * b + 2, 2)
+        load_order = [("chunk", k) for k in range(PACK)]
+        for k in range(len(x2_list)):
+            load_order.extend([("copy", k), ("chunk", PACK + k)])
+        progress = {"loads": 0, "copy": 0, "chunk": 0}
+        room = {"copy": X2_SLOTS, "chunk": X_SLOTS}
 
-        load_chunks(0, PACK)
-        load_image(1)
+        def write_loads():
+            for n in range(progress["loads"], len(load_order)):
+                kind, k = load_order[n]
+                if k >= room[kind] + progress[kind]:
+                    return
+                if kind == "copy":
+                    load_x2(k, 1)
+                else:
+                    load_chunks(k, 1)
+                progress["loads"] = n + 1
+
+        write_loads()
 
         one = const.tile([P, 1], F32)
         nc.vector.memset(one[:], 1.0)
         table_warm = const.tile([P, 1], F32)
         nc.scalar.activation(out=table_warm[:], in_=one[:], func=ACT.Sqrt)
-        eps_share = const.tile([P, 1], F32)
-        nc.vector.memset(eps_share[:], EPS / PACK)
+        eps_share = {}
+        for columns in (PACK, PACK + 1):
+            eps_share[columns] = const.tile([P, 1], F32, name="eps_share%d" % columns)
+            nc.vector.memset(eps_share[columns][:], EPS / columns)
 
         class_mask = const.tile([P, CLASSES], BF16)
         nc.gpsimd.memset(class_mask[:], 1.0)
@@ -176,8 +190,12 @@ def tile_multihead_attn_pa_t_kernel(tc, X, gn_w, gn_b, kqv_w, kqv_b, out):
             )
 
         def later_pivot(b):
-            sum_pivot = stat.tile([P, 1], F32, name="sum_pivot")
-            pivot(b, sum_pivot[:])
+            neg_pivot[b] = stat.tile([P, 1], F32, name="neg_pivot")
+            junk = junk_pool.tile([P, PIVOT_PIXELS], BF16, name="junk")
+            nc.vector.tensor_scalar(
+                out=junk[:], in0=x_chunk[(b, 0)][:, :PIVOT_PIXELS], scalar1=-1.0 / PIVOT_PIXELS,
+                scalar2=None, op0=ALU.mult, op1=ALU.add, accum_out=neg_pivot[b][:],
+            )
 
         def square_on_scalar(b, j, width):
             unread_s = unread_s_pool.tile([P, PIXELS], BF16, name="unread_s")
@@ -192,13 +210,19 @@ def tile_multihead_attn_pa_t_kernel(tc, X, gn_w, gn_b, kqv_w, kqv_b, out):
                 square_on_scalar(b, j, PIXELS)
 
         sum_x0 = const.tile([P, PACK + 1], F32)
-        sum_sq[0] = stat.tile([P, PACK], F32, name="sum_sq")
-        pivot(0, sum_x0[:, 0:1])
-        sum_on_vector(x_chunk[(0, 0)], PIVOT_PIXELS, PIXELS, sum_x0[:, 1:2])
-        square_on_scalar(0, 0, PIXELS)
-        sum_on_vector(x_chunk[(0, 1)], 0, PIXELS, sum_x0[:, 2:3])
-        square_on_scalar(0, 1, PIXELS)
+        sum_sq0 = const.tile([P, PACK + 1], F32)
+        sum_sq[0] = sum_sq0
+        bn_out = const.tile([P, PACK * BN_PER_CHUNK, 6], F32)
+        ident_bf = const.tile([P, P], BF16)
+        masks.make_identity(nc, ident_bf[:])
+        folded = psum_s.tile([P, 512], F32, name="part_sums")
+        fold_list = [
+            (j, c)
+            for j in range(1, PACK)
+            for c in range((HEAD_SCALAR if j < PACK - 1 else HEAD_FOLD_3) // P)
+        ]
 
+        pivot(0, sum_x0[:, 0:1])
         gain = const.tile([P, PACK], F32)
         nc.vector.tensor_copy(out=gain[:], in_=gain_bf[:])
         neg_gain_over_n = const.tile([P, PACK], F32)
@@ -211,22 +235,31 @@ def tile_multihead_attn_pa_t_kernel(tc, X, gn_w, gn_b, kqv_w, kqv_b, out):
         bias = const.tile([P, M_TILES], F32)
         nc.vector.tensor_copy(out=bias[:], in_=bias_bf[:])
 
-        sum_on_vector(x_chunk[(0, 2)], 0, HEAD_SPLIT, sum_x0[:, 3:4])
-        square_on_scalar(0, 2, HEAD_SPLIT)
-        bn_out = const.tile([P, BN_PIECES, 6], F32)
-        for i in range(BN_PIECES):
-            first = HEAD_SPLIT + i * BN_WIDTH
-            nc.vector.bn_stats(
-                out=bn_out[:, i, :],
-                in_=x_chunk[(0, 2 + first // PIXELS)][:, first % PIXELS : first % PIXELS + BN_WIDTH],
+        for j in range(PACK):
+            square_on_scalar(0, j, HEAD_SCALAR)
+            for i in range(BN_PER_CHUNK):
+                first = HEAD_SCALAR + i * BN_WIDTH
+                nc.vector.bn_stats(
+                    out=bn_out[:, j * BN_PER_CHUNK + i, :],
+                    in_=x_chunk[(0, j)][:, first : first + BN_WIDTH],
+                )
+            if j == 0:
+                sum_on_vector(x_chunk[(0, 0)], PIVOT_PIXELS, HEAD_SCALAR, sum_x0[:, 1:2])
+            if j == PACK - 1:
+                sum_on_vector(x_chunk[(0, j)], HEAD_FOLD_3, HEAD_SCALAR, sum_x0[:, 2:3])
+        for n in range(len(fold_list)):
+            j, c = fold_list[n]
+            nc.tensor.matmul(
+                out=folded[:, :P], lhsT=ident_bf[:], rhs=x_chunk[(0, j)][:, c * P : (c + 1) * P],
+                start=(n == 0), stop=(n == len(fold_list) - 1),
             )
-            if i == BN_PIECES // 2:
-                later_pivot(1)
+        later_pivot(1)
+        nc.vector.reduce_sum(out=sum_x0[:, 3:4], in_=folded[:, :P], axis=AXIS.X)
         mean_var = const.tile([P, 2], F32)
         nc.vector.bn_aggr(out=mean_var[:], in_=bn_out[:].rearrange("p i s -> p (i s)"))
         nc.vector.tensor_scalar(
-            out=sum_x0[:, 4:5], in0=mean_var[:, 0:1], scalar1=float(BN_PIECES * BN_WIDTH),
-            scalar2=None, op0=ALU.mult,
+            out=sum_x0[:, 4:5], in0=mean_var[:, 0:1], scalar1=float(BN_VALUES), scalar2=None,
+            op0=ALU.mult,
         )
         off_pivot = const.tile([P, 1], F32)
         nc.vector.tensor_scalar(
@@ -239,11 +272,12 @@ def tile_multihead_attn_pa_t_kernel(tc, X, gn_w, gn_b, kqv_w, kqv_b, out):
             op0=ALU.mult, op1=ALU.add,
         )
         nc.vector.tensor_scalar(
-            out=sum_sq[0][:, 3:4], in0=mean_sq_off[:], scalar1=float(BN_PIECES * BN_WIDTH),
+            out=sum_sq0[:, PACK : PACK + 1], in0=mean_sq_off[:], scalar1=float(BN_VALUES),
             scalar2=None, op0=ALU.mult,
         )
-        total_x[0] = stat.tile([P, 1], F32, name="total_x")
-        nc.vector.reduce_sum(out=total_x[0][:], in_=sum_x0[:], axis=AXIS.X)
+        total_x0 = const.tile([P, 1], F32)
+        nc.vector.reduce_sum(out=total_x0[:], in_=sum_x0[:], axis=AXIS.X)
+        total_x[0] = total_x0[:]
 
         part_sums = {}
 
@@ -261,17 +295,14 @@ def tile_multihead_attn_pa_t_kernel(tc, X, gn_w, gn_b, kqv_w, kqv_b, out):
                         start=(c == 0),
                         stop=(c == RUN // P - 1),
                     )
+            progress["copy"] = i + 1
+            write_loads()
 
         def gather_total(b):
             part = part_pool.tile([P, P], F32, name="part")
             nc.vector.tensor_copy(out=part[:], in_=part_sums[b][:, :P])
-            nc.tensor.matmul(
-                out=part_sums[b][:, P : P + 1], lhsT=part[:], rhs=one[:], start=True, stop=True
-            )
-
-        def read_total(b):
-            total_x[b] = stat.tile([P, 1], F32, name="total_x")
-            nc.vector.tensor_copy(out=total_x[b][:], in_=part_sums[b][:, P : P + 1])
+            total_x[b] = part_sums[b][:, P : P + 1]
+            nc.tensor.matmul(out=total_x[b], lhsT=part[:], rhs=one[:], start=True, stop=True)
 
         neg_mean_gain = {}
         std = {}
@@ -279,19 +310,20 @@ def tile_multihead_attn_pa_t_kernel(tc, X, gn_w, gn_b, kqv_w, kqv_b, out):
         def moments(b):
             neg_mean_gain[b] = stat.tile([P, PACK], F32, name="neg_mean_gain")
             nc.vector.tensor_scalar(
-                out=neg_mean_gain[b][:], in0=neg_gain_over_n[:], scalar1=total_x[b][:, 0:1],
+                out=neg_mean_gain[b][:], in0=neg_gain_over_n[:], scalar1=total_x[b],
                 scalar2=None, op0=ALU.mult,
             )
             offset_sq = stat.tile([P, 1], F32, name="offset_sq")
             nc.scalar.activation(
-                out=offset_sq[:], in_=total_x[b][:], func=ACT.Square, bias=neg_pivot[b][:, 0:1],
+                out=offset_sq[:], in_=total_x[b], func=ACT.Square, bias=neg_pivot[b][:, 0:1],
                 scale=1.0 / GROUP_SIZE,
             )
-            sq_share = stat.tile([P, PACK], F32, name="sq_share")
+            columns = sum_sq[b][:].shape[1]
+            sq_share = stat.tile([P, PACK + 1], F32, name="sq_share")
             mean_sq_eps = stat.tile([P, 1], F32, name="mean_sq_eps")
             nc.scalar.activation(
-                out=sq_share[:], in_=sum_sq[b][:], func=ACT.Identity, bias=eps_share[:, 0:1],
-                scale=1.0 / GROUP_SIZE, accum_out=mean_sq_eps[:],
+                out=sq_share[:, :columns], in_=sum_sq[b][:], func=ACT.Identity,
+                bias=eps_share[columns][:, 0:1], scale=1.0 / GROUP_SIZE, accum_out=mean_sq_eps[:],
             )
             std[b] = stat.tile([P, 1], F32, name="std")
             nc.scalar.activation(
@@ -317,8 +349,8 @@ def tile_multihead_attn_pa_t_kernel(tc, X, gn_w, gn_b, kqv_w, kqv_b, out):
                     in0=x_chunk[(b, j)][:].rearrange("p (i th w) -> p th i w", th=POOL, w=SIDE),
                     scalar1=a[:, j : j + 1], scalar2=c[:, j : j + 1], op0=ALU.mult, op1=ALU.add,
                 )
-            if b + 2 < BATCH:
-                load_image(b + 2)
+            progress["chunk"] = PACK * (b + 1)
+            write_loads()
             return y
 
         def regroup(copy, g, y, th):
@@ -353,13 +385,15 @@ def tile_multihead_attn_pa_t_kernel(tc, X, gn_w, gn_b, kqv_w, kqv_b, out):
                         stop=(th == POOL - 1 and tw == POOL - 1),
                     )
 
-        def leave_on_scalar(b, acc):
+        def leave_on_scalar(b, acc, m):
             res0 = res_pool.tile([P, CELLS], F32, name="res0")
             nc.scalar.activation(
-                out=res0[:], in_=acc[0][:], func=ACT.Identity, bias=bias[:, 0:1],
+                out=res0[:], in_=acc[m][:], func=ACT.Identity, bias=bias[:, m : m + 1],
                 scale=1.0 / (POOL * POOL),
             )
-            nc.scalar.dma_start(out=out[b, 0:P].rearrange("o i jj -> o (i jj)"), in_=res0[:])
+            nc.sync.dma_start(
+                out=out[b, m * P : (m + 1) * P].rearrange("o i jj -> o (i jj)"), in_=res0[:]
+            )
 
         def leave_on_vector(b, acc):
             res1 = res_pool.tile([P, CELLS], F32, name="res1")
@@ -382,21 +416,19 @@ def tile_multihead_attn_pa_t_kernel(tc, X, gn_w, gn_b, kqv_w, kqv_b, out):
             if b == BATCH - 1:
                 for th in range(first_scalar, POOL):
                     g[th] = regroup_on_scalar(y, th)
-            if b > 0:
-                leave_on_scalar(b - 1, acc_done)
             acc = [psum.tile([P, CELLS], F32, name="acc%d" % m) for m in range(M_TILES)]
             for th in range(POOL):
                 if th < first_scalar:
                     g[th] = regroup_on_vector(y, th)
                 if th == 0 and b == 0:
                     quantise_weights()
-                    gather_total(1)
-                if th == 0 and b > 0:
-                    leave_on_vector(b - 1, acc_done)
-                if th == 1 and b + 1 < BATCH:
-                    read_total(b + 1)
-                if b + 2 < BATCH:
-                    sum_on_tensor(LOADS * (b + 1) + th)
+                if th == 2 and b > 0:
+                    for m in range(M_TILES):
+                        leave_on_scalar(b - 1, acc_done, m)
+                if th == 2 and b + 1 < BATCH:
+                    gather_total(b + 1)
+                if LOADS <= POOL * b + th + 2 < len(x2_list):
+                    sum_on_tensor(POOL * b + th + 2)
                 if th == POOL - 1 and b + 1 < BATCH:
                     moments(b + 1)
                     if b + 2 < BATCH:
@@ -409,8 +441,6 @@ def tile_multihead_attn_pa_t_kernel(tc, X, gn_w, gn_b, kqv_w, kqv_b, out):
                 if th == 2 and b + 2 < BATCH:
                     later_pivot(b + 2)
             quantise_and_multiply(g[POOL - 1], acc, POOL - 1)
-            if b + 2 < BATCH:
-                gather_total(b + 2)
             acc_done = acc
-        leave_on_scalar(BATCH - 1, acc_done)
+        leave_on_scalar(BATCH - 1, acc_done, 0)
         leave_on_vector(BATCH - 1, acc_done)

@@ -28,18 +28,18 @@ EPS = 1e-5
 PIVOT_PIXELS = 256
 X_SLOTS = 8
 PE_SUM_FROM = 1
-SLABS = 8
-RUN = 2048
-PARTS_OF_GROUP = 8
-CLASSES = 16
-SLABS_PER_LOAD = 2
+SLABS = 16
+RUN = 1024
+PARTS_OF_GROUP = 16
+CLASSES = 8
+SLABS_PER_LOAD = 4
 X2_SLOTS = 4
 SCALAR_CLASSES = (0, 0, 1, 2)
-HEAD_SCALAR = 2560
-HEAD_FOLD_3 = 1024
+HEAD_SCALAR = (2560, 2560, 2560, 3072)
+HEAD_FOLD_3 = 1536
+HEAD_FIRST = 1024
 BN_WIDTH = 512
-BN_PER_CHUNK = (PIXELS - HEAD_SCALAR) // BN_WIDTH
-BN_VALUES = PACK * BN_PER_CHUNK * BN_WIDTH
+BN_VALUES = PACK * PIXELS - sum(HEAD_SCALAR)
 
 FLOPS = 2 * BATCH * OUT_CH * CHANNELS * PIXELS
 
@@ -84,11 +84,15 @@ def tile_multihead_attn_pa_t_kernel(tc, X, gn_w, gn_b, kqv_w, kqv_b, out):
                 b, j = divmod(k, PACK)
                 pixels = X[b].rearrange("(p j) h w -> p j (h w)", j=PACK)[:, j, :]
                 x_bj = x_pool.tile([P, PIXELS], BF16, name="x_bj")
+                cuts = [0, PIXELS]
                 if j == 0:
-                    nc.sync.dma_start(out=x_bj[:, :PIVOT_PIXELS], in_=pixels[:, :PIVOT_PIXELS])
-                    nc.sync.dma_start(out=x_bj[:, PIVOT_PIXELS:], in_=pixels[:, PIVOT_PIXELS:])
-                else:
-                    nc.sync.dma_start(out=x_bj[:], in_=pixels)
+                    cuts = [0, PIVOT_PIXELS, PIXELS]
+                if k == 0:
+                    cuts = [0, PIVOT_PIXELS, HEAD_FIRST, PIXELS]
+                for n in range(len(cuts) - 1):
+                    nc.sync.dma_start(
+                        out=x_bj[:, cuts[n] : cuts[n + 1]], in_=pixels[:, cuts[n] : cuts[n + 1]]
+                    )
                 x_chunk[(b, j)] = x_bj
 
         LOADS = SLABS // SLABS_PER_LOAD
@@ -131,7 +135,7 @@ def tile_multihead_attn_pa_t_kernel(tc, X, gn_w, gn_b, kqv_w, kqv_b, out):
         table_warm = const.tile([P, 1], F32)
         nc.scalar.activation(out=table_warm[:], in_=one[:], func=ACT.Sqrt)
         eps_share = {}
-        for columns in (PACK, PACK + 1):
+        for columns in (PACK, PACK + 2):
             eps_share[columns] = const.tile([P, 1], F32, name="eps_share%d" % columns)
             nc.vector.memset(eps_share[columns][:], EPS / columns)
 
@@ -158,10 +162,6 @@ def tile_multihead_attn_pa_t_kernel(tc, X, gn_w, gn_b, kqv_w, kqv_b, out):
         w_scales = const.tile([P, OUT_CH], U8, align_bytes=64)
 
         def quantise_weights():
-            nc.vector.tensor_copy(
-                out=w_grouped[:].bitcast(F32).rearrange("p (o u) -> p o u", u=2),
-                in_=w_t[:].rearrange("p u o -> p o u"),
-            )
             nc.vector.quantize_mx(
                 out=w_codes[:].bitcast(FP8X4), scales=w_scales[:], in_=w_grouped[:]
             )
@@ -197,29 +197,32 @@ def tile_multihead_attn_pa_t_kernel(tc, X, gn_w, gn_b, kqv_w, kqv_b, out):
                 scalar2=None, op0=ALU.mult, op1=ALU.add, accum_out=neg_pivot[b][:],
             )
 
-        def square_on_scalar(b, j, width):
+        def square_on_scalar(b, j, first, end, column):
             unread_s = unread_s_pool.tile([P, PIXELS], BF16, name="unread_s")
             nc.scalar.activation(
-                out=unread_s[:, :width], in_=x_chunk[(b, j)][:, :width], func=ACT.Square,
-                bias=neg_pivot[b][:, 0:1], scale=1.0, accum_out=sum_sq[b][:, j : j + 1],
+                out=unread_s[:, first:end], in_=x_chunk[(b, j)][:, first:end], func=ACT.Square,
+                bias=neg_pivot[b][:, 0:1], scale=1.0, accum_out=sum_sq[b][:, column : column + 1],
             )
 
         def squares(b):
             sum_sq[b] = stat.tile([P, PACK], F32, name="sum_sq")
             for j in range(PACK):
-                square_on_scalar(b, j, PIXELS)
+                square_on_scalar(b, j, 0, PIXELS, j)
 
-        sum_x0 = const.tile([P, PACK + 1], F32)
-        sum_sq0 = const.tile([P, PACK + 1], F32)
+        sum_x0 = const.tile([P, PACK], F32)
+        sum_sq0 = const.tile([P, PACK + 2], F32)
         sum_sq[0] = sum_sq0
-        bn_out = const.tile([P, PACK * BN_PER_CHUNK, 6], F32)
+        bn_out = const.tile([P, BN_VALUES // BN_WIDTH, 6], F32)
         ident_bf = const.tile([P, P], BF16)
         masks.make_identity(nc, ident_bf[:])
         folded = psum_s.tile([P, 512], F32, name="part_sums")
         fold_list = [
             (j, c)
-            for j in range(1, PACK)
-            for c in range((HEAD_SCALAR if j < PACK - 1 else HEAD_FOLD_3) // P)
+            for j in range(PACK)
+            for c in range(
+                PIVOT_PIXELS // P if j == 0 else 0,
+                (HEAD_SCALAR[j] if j < PACK - 1 else HEAD_FOLD_3) // P,
+            )
         ]
 
         pivot(0, sum_x0[:, 0:1])
@@ -235,18 +238,24 @@ def tile_multihead_attn_pa_t_kernel(tc, X, gn_w, gn_b, kqv_w, kqv_b, out):
         bias = const.tile([P, M_TILES], F32)
         nc.vector.tensor_copy(out=bias[:], in_=bias_bf[:])
 
+        pieces = 0
         for j in range(PACK):
-            square_on_scalar(0, j, HEAD_SCALAR)
-            for i in range(BN_PER_CHUNK):
-                first = HEAD_SCALAR + i * BN_WIDTH
-                nc.vector.bn_stats(
-                    out=bn_out[:, j * BN_PER_CHUNK + i, :],
-                    in_=x_chunk[(0, j)][:, first : first + BN_WIDTH],
-                )
             if j == 0:
-                sum_on_vector(x_chunk[(0, 0)], PIVOT_PIXELS, HEAD_SCALAR, sum_x0[:, 1:2])
+                square_on_scalar(0, 0, 0, HEAD_FIRST, PACK)
+                nc.scalar.copy(
+                    out=w_grouped[:].bitcast(F32).rearrange("p (o u) -> p o u", u=2),
+                    in_=w_t[:].rearrange("p u o -> p o u"),
+                )
+                square_on_scalar(0, 0, HEAD_FIRST, HEAD_SCALAR[0], 0)
+            else:
+                square_on_scalar(0, j, 0, HEAD_SCALAR[j], j)
+            for first in range(HEAD_SCALAR[j], PIXELS, BN_WIDTH):
+                nc.vector.bn_stats(
+                    out=bn_out[:, pieces, :], in_=x_chunk[(0, j)][:, first : first + BN_WIDTH]
+                )
+                pieces = pieces + 1
             if j == PACK - 1:
-                sum_on_vector(x_chunk[(0, j)], HEAD_FOLD_3, HEAD_SCALAR, sum_x0[:, 2:3])
+                sum_on_vector(x_chunk[(0, j)], HEAD_FOLD_3, HEAD_SCALAR[j], sum_x0[:, 1:2])
         for n in range(len(fold_list)):
             j, c = fold_list[n]
             nc.tensor.matmul(
@@ -254,11 +263,11 @@ def tile_multihead_attn_pa_t_kernel(tc, X, gn_w, gn_b, kqv_w, kqv_b, out):
                 start=(n == 0), stop=(n == len(fold_list) - 1),
             )
         later_pivot(1)
-        nc.vector.reduce_sum(out=sum_x0[:, 3:4], in_=folded[:, :P], axis=AXIS.X)
+        nc.vector.reduce_sum(out=sum_x0[:, 2:3], in_=folded[:, :P], axis=AXIS.X)
         mean_var = const.tile([P, 2], F32)
         nc.vector.bn_aggr(out=mean_var[:], in_=bn_out[:].rearrange("p i s -> p (i s)"))
         nc.vector.tensor_scalar(
-            out=sum_x0[:, 4:5], in0=mean_var[:, 0:1], scalar1=float(BN_VALUES), scalar2=None,
+            out=sum_x0[:, 3:4], in0=mean_var[:, 0:1], scalar1=float(BN_VALUES), scalar2=None,
             op0=ALU.mult,
         )
         off_pivot = const.tile([P, 1], F32)
@@ -272,7 +281,7 @@ def tile_multihead_attn_pa_t_kernel(tc, X, gn_w, gn_b, kqv_w, kqv_b, out):
             op0=ALU.mult, op1=ALU.add,
         )
         nc.vector.tensor_scalar(
-            out=sum_sq0[:, PACK : PACK + 1], in0=mean_sq_off[:], scalar1=float(BN_VALUES),
+            out=sum_sq0[:, PACK + 1 : PACK + 2], in0=mean_sq_off[:], scalar1=float(BN_VALUES),
             scalar2=None, op0=ALU.mult,
         )
         total_x0 = const.tile([P, 1], F32)
@@ -319,7 +328,7 @@ def tile_multihead_attn_pa_t_kernel(tc, X, gn_w, gn_b, kqv_w, kqv_b, out):
                 scale=1.0 / GROUP_SIZE,
             )
             columns = sum_sq[b][:].shape[1]
-            sq_share = stat.tile([P, PACK + 1], F32, name="sq_share")
+            sq_share = stat.tile([P, PACK + 2], F32, name="sq_share")
             mean_sq_eps = stat.tile([P, 1], F32, name="mean_sq_eps")
             nc.scalar.activation(
                 out=sq_share[:, :columns], in_=sum_sq[b][:], func=ACT.Identity,

@@ -28,15 +28,15 @@ EPS = 1e-5
 PIVOT_PIXELS = 256
 X_SLOTS = 8
 PE_SUM_FROM = 1
-SLABS = 16
-RUN = 1024
-PARTS_OF_GROUP = 16
-CLASSES = 8
-SLABS_PER_LOAD = 4
+SLABS = 8
+RUN = 2048
+PARTS_OF_GROUP = 8
+CLASSES = 16
+SLABS_PER_LOAD = 2
 X2_SLOTS = 4
 SCALAR_CLASSES = (0, 0, 1, 2)
-HEAD_SCALAR = (2560, 2560, 2560, 3072)
-HEAD_FOLD_3 = 1536
+HEAD_SCALAR = (2560, 2560, 3072, 3072)
+HEAD_FOLD_3 = 512
 HEAD_FIRST = 1024
 BN_WIDTH = 512
 BN_VALUES = PACK * PIXELS - sum(HEAD_SCALAR)
@@ -209,7 +209,7 @@ def tile_multihead_attn_pa_t_kernel(tc, X, gn_w, gn_b, kqv_w, kqv_b, out):
             for j in range(PACK):
                 square_on_scalar(b, j, 0, PIXELS, j)
 
-        sum_x0 = const.tile([P, PACK], F32)
+        sum_x0 = const.tile([P, PACK + 1], F32)
         sum_sq0 = const.tile([P, PACK + 2], F32)
         sum_sq[0] = sum_sq0
         bn_out = const.tile([P, BN_VALUES // BN_WIDTH, 6], F32)
@@ -218,11 +218,8 @@ def tile_multihead_attn_pa_t_kernel(tc, X, gn_w, gn_b, kqv_w, kqv_b, out):
         folded = psum_s.tile([P, 512], F32, name="part_sums")
         fold_list = [
             (j, c)
-            for j in range(PACK)
-            for c in range(
-                PIVOT_PIXELS // P if j == 0 else 0,
-                (HEAD_SCALAR[j] if j < PACK - 1 else HEAD_FOLD_3) // P,
-            )
+            for j in range(1, PACK)
+            for c in range((HEAD_SCALAR[j] if j < PACK - 1 else HEAD_FOLD_3) // P)
         ]
 
         pivot(0, sum_x0[:, 0:1])
@@ -254,6 +251,8 @@ def tile_multihead_attn_pa_t_kernel(tc, X, gn_w, gn_b, kqv_w, kqv_b, out):
                     out=bn_out[:, pieces, :], in_=x_chunk[(0, j)][:, first : first + BN_WIDTH]
                 )
                 pieces = pieces + 1
+            if j == 0:
+                sum_on_vector(x_chunk[(0, 0)], PIVOT_PIXELS, HEAD_SCALAR[0], sum_x0[:, 4:5])
             if j == PACK - 1:
                 sum_on_vector(x_chunk[(0, j)], HEAD_FOLD_3, HEAD_SCALAR[j], sum_x0[:, 1:2])
         for n in range(len(fold_list)):

@@ -112,8 +112,10 @@ def tile_multihead_attn_pa_t_kernel(tc, X, gn_w, gn_b, kqv_w, kqv_b, out):
                 x2_tile[i] = x2
 
         load_order = [("chunk", k) for k in range(PACK)]
-        for k in range(len(x2_list)):
+        for k in range(len(x2_list) - LOADS):
             load_order.extend([("copy", k), ("chunk", PACK + k)])
+        load_order.extend([("chunk", PACK * (BATCH - 1) + j) for j in range(PACK)])
+        load_order.extend([("copy", len(x2_list) - LOADS + h) for h in range(LOADS)])
         progress = {"loads": 0, "copy": 0, "chunk": 0}
         room = {"copy": X2_SLOTS, "chunk": X_SLOTS}
 
@@ -435,8 +437,11 @@ def tile_multihead_attn_pa_t_kernel(tc, X, gn_w, gn_b, kqv_w, kqv_b, out):
                         leave_on_scalar(b - 1, acc_done, m)
                 if th == 2 and b + 1 < BATCH:
                     gather_total(b + 1)
-                if LOADS <= POOL * b + th + 2 < len(x2_list):
+                if LOADS <= POOL * b + th + 2 < 2 * LOADS:
                     sum_on_tensor(POOL * b + th + 2)
+                if b == BATCH - 2 and th < 2:
+                    sum_on_tensor(2 * LOADS + 2 * th)
+                    sum_on_tensor(2 * LOADS + 2 * th + 1)
                 if th == POOL - 1 and b + 1 < BATCH:
                     moments(b + 1)
                     if b + 2 < BATCH:

@@ -53,9 +53,8 @@ def tile_multihead_attn_pa_t_kernel(tc, X, gn_w, gn_b, kqv_w, kqv_b, out):
         junk_pool = ctx.enter_context(tc.tile_pool(name="junk", bufs=1))
         part_pool = ctx.enter_context(tc.tile_pool(name="part", bufs=2))
         y_pool = ctx.enter_context(tc.tile_pool(name="y", bufs=2))
-        v_pool = ctx.enter_context(tc.tile_pool(name="v_out", bufs=2))
+        v_pool = ctx.enter_context(tc.tile_pool(name="v_out", bufs=3))
         g_s_pool = ctx.enter_context(tc.tile_pool(name="g_s", bufs=2))
-        unread_s_pool = ctx.enter_context(tc.tile_pool(name="unread_s", bufs=1))
         q_pool = ctx.enter_context(tc.tile_pool(name="q", bufs=3))
         stat = ctx.enter_context(tc.tile_pool(name="stat", bufs=BATCH))
         res_pool = ctx.enter_context(tc.tile_pool(name="res", bufs=2))
@@ -200,7 +199,7 @@ def tile_multihead_attn_pa_t_kernel(tc, X, gn_w, gn_b, kqv_w, kqv_b, out):
             )
 
         def square_on_scalar(b, j, first, end, column):
-            unread_s = unread_s_pool.tile([P, PIXELS], BF16, name="unread_s")
+            unread_s = g_s_pool.tile([P, PIXELS], BF16, name="unread_s", tag="g_s", align_bytes=64)
             nc.scalar.activation(
                 out=unread_s[:, first:end], in_=x_chunk[(b, j)][:, first:end], func=ACT.Square,
                 bias=neg_pivot[b][:, 0:1], scale=1.0, accum_out=sum_sq[b][:, column : column + 1],
@@ -371,7 +370,7 @@ def tile_multihead_attn_pa_t_kernel(tc, X, gn_w, gn_b, kqv_w, kqv_b, out):
             return g
 
         def regroup_on_scalar(y, th):
-            g_s = g_s_pool.tile([P, PIXELS], BF16, name="g_s", align_bytes=64)
+            g_s = g_s_pool.tile([P, PIXELS], BF16, name="g_s", tag="g_s", align_bytes=64)
             return regroup(nc.scalar.copy, g_s, y, th)
 
         def regroup_on_vector(y, th):

@@ -57,7 +57,7 @@ def tile_multihead_attn_pa_t_kernel(tc, X, gn_w, gn_b, kqv_w, kqv_b, out):
         g_s_pool = ctx.enter_context(tc.tile_pool(name="g_s", bufs=2))
         q_pool = ctx.enter_context(tc.tile_pool(name="q", bufs=3))
         stat = ctx.enter_context(tc.tile_pool(name="stat", bufs=BATCH))
-        res_pool = ctx.enter_context(tc.tile_pool(name="res", bufs=2))
+        res_pool = ctx.enter_context(tc.tile_pool(name="res", bufs=4))
         psum_w = ctx.enter_context(tc.psum_pool(name="psum_w", bufs=1))
         psum = ctx.enter_context(tc.psum_pool(name="psum", bufs=2))
         psum_s = ctx.enter_context(tc.psum_pool(name="psum_s", bufs=2))
@@ -339,18 +339,27 @@ def tile_multihead_attn_pa_t_kernel(tc, X, gn_w, gn_b, kqv_w, kqv_b, out):
                 out=std[b][:], in_=offset_sq[:], func=ACT.Sqrt, bias=mean_sq_eps[:, 0:1], scale=-1.0
             )
 
-        def normalise(b):
-            rstd = stat.tile([P, 1], F32, name="rstd")
-            nc.vector.reciprocal(out=rstd[:], in_=std[b][:])
+        rstd = {}
+        factors = {}
+
+        def invert_std(b):
+            rstd[b] = stat.tile([P, 1], F32, name="rstd")
+            nc.vector.reciprocal(out=rstd[b][:], in_=std[b][:])
+
+        def gain_and_shift(b):
             a = stat.tile([P, PACK], F32, name="a")
             nc.vector.tensor_scalar(
-                out=a[:], in0=gain[:], scalar1=rstd[:, 0:1], scalar2=None, op0=ALU.mult
+                out=a[:], in0=gain[:], scalar1=rstd[b][:, 0:1], scalar2=None, op0=ALU.mult
             )
             c = stat.tile([P, PACK], F32, name="c")
             nc.vector.scalar_tensor_tensor(
-                out=c[:], in0=neg_mean_gain[b][:], scalar=rstd[:, 0:1], in1=shift[:],
+                out=c[:], in0=neg_mean_gain[b][:], scalar=rstd[b][:, 0:1], in1=shift[:],
                 op0=ALU.mult, op1=ALU.add,
             )
+            factors[b] = (a, c)
+
+        def normalise(b):
+            a, c = factors[b]
             y = y_pool.tile([P, POOL, PACK, ROW_CLASS], BF16, name="y")
             for j in range(PACK):
                 nc.vector.tensor_scalar(
@@ -377,12 +386,21 @@ def tile_multihead_attn_pa_t_kernel(tc, X, gn_w, gn_b, kqv_w, kqv_b, out):
             g_v = v_pool.tile([P, PIXELS], BF16, name="g_v", tag="v_out", align_bytes=64)
             return regroup(nc.vector.tensor_copy, g_v, y, th)
 
-        def quantise_and_multiply(g, acc, th):
-            codes = q_pool.tile([P, POOL * CELLS], U32, name="codes", align_bytes=64)
-            scales = q_pool.tile([P, POOL * CELLS], U8, name="scales", align_bytes=64)
-            nc.vector.quantize_mx(out=codes[:].bitcast(FP8X4), scales=scales[:], in_=g[:])
+        q_tiles = {}
+
+        def quantise_and_multiply(g, acc, th, first_plane=0, planes=POOL):
+            if first_plane == 0:
+                codes = q_pool.tile([P, POOL * CELLS], U32, name="codes", align_bytes=64)
+                scales = q_pool.tile([P, POOL * CELLS], U8, name="scales", align_bytes=64)
+                q_tiles[th] = (codes, scales)
+            codes, scales = q_tiles[th]
+            part = slice(first_plane * CELLS, (first_plane + planes) * CELLS)
+            nc.vector.quantize_mx(
+                out=codes[:, part].bitcast(FP8X4), scales=scales[:, part],
+                in_=g[:, first_plane * CELLS * PACK : (first_plane + planes) * CELLS * PACK],
+            )
             for m in range(M_TILES):
-                for tw in range(POOL):
+                for tw in range(first_plane, first_plane + planes):
                     plane = slice(tw * CELLS, (tw + 1) * CELLS)
                     nc.tensor.matmul_mx(
                         out=acc[m][:],
@@ -416,6 +434,9 @@ def tile_multihead_attn_pa_t_kernel(tc, X, gn_w, gn_b, kqv_w, kqv_b, out):
         squares(1)
         for i in range(LOADS):
             sum_on_tensor(i)
+        quantise_weights()
+        invert_std(0)
+        gain_and_shift(0)
         y_next = normalise(0)
         acc_done = None
         for b in range(BATCH):
@@ -429,8 +450,6 @@ def tile_multihead_attn_pa_t_kernel(tc, X, gn_w, gn_b, kqv_w, kqv_b, out):
             for th in range(POOL):
                 if th < first_scalar:
                     g[th] = regroup_on_vector(y, th)
-                if th == 0 and b == 0:
-                    quantise_weights()
                 if th == 2 and b > 0:
                     for m in range(M_TILES):
                         leave_on_scalar(b - 1, acc_done, m)
@@ -447,12 +466,22 @@ def tile_multihead_attn_pa_t_kernel(tc, X, gn_w, gn_b, kqv_w, kqv_b, out):
                         squares(b + 2)
                     for late in range(first_scalar, POOL):
                         g[late] = regroup_on_scalar(y, late)
+                    invert_std(b + 1)
+                    quantise_and_multiply(g[2], acc, 2)
+                    gain_and_shift(b + 1)
+                    if first_scalar == POOL:
+                        quantise_and_multiply(g[3], acc, 3, 0, 2)
                     y_next = normalise(b + 1)
-                if th > 0:
+                    if first_scalar == POOL:
+                        quantise_and_multiply(g[3], acc, 3, 2, 2)
+                    else:
+                        quantise_and_multiply(g[3], acc, 3)
+                elif th > 0:
                     quantise_and_multiply(g[th - 1], acc, th - 1)
                 if th == 2 and b + 2 < BATCH:
                     later_pivot(b + 2)
-            quantise_and_multiply(g[POOL - 1], acc, POOL - 1)
+            if b == BATCH - 1:
+                quantise_and_multiply(g[POOL - 1], acc, POOL - 1)
             acc_done = acc
         leave_on_scalar(BATCH - 1, acc_done, 0)
         leave_on_vector(BATCH - 1, acc_done)

@@ -192,10 +192,10 @@ def tile_multihead_attn_pa_t_kernel(tc, X, gn_w, gn_b, kqv_w, kqv_b, out):
 
         def later_pivot(b):
             neg_pivot[b] = stat.tile([P, 1], F32, name="neg_pivot")
-            junk = junk_pool.tile([P, PIVOT_PIXELS], BF16, name="junk")
-            nc.vector.tensor_scalar(
-                out=junk[:], in0=x_chunk[(b, 0)][:, :PIVOT_PIXELS], scalar1=-1.0 / PIVOT_PIXELS,
-                scalar2=None, op0=ALU.mult, op1=ALU.add, accum_out=neg_pivot[b][:],
+            junk_s = junk_pool.tile([P, PIVOT_PIXELS], BF16, name="junk_s")
+            nc.scalar.activation(
+                out=junk_s[:], in_=x_chunk[(b, 0)][:, :PIVOT_PIXELS], func=ACT.Identity,
+                scale=-1.0 / PIVOT_PIXELS, accum_out=neg_pivot[b][:],
             )
 
         def square_on_scalar(b, j, first, end, column):
@@ -224,15 +224,16 @@ def tile_multihead_attn_pa_t_kernel(tc, X, gn_w, gn_b, kqv_w, kqv_b, out):
         ]
 
         pivot(0, sum_x0[:, 0:1])
-        gain = const.tile([P, PACK], F32)
-        nc.vector.tensor_copy(out=gain[:], in_=gain_bf[:])
+        gain_mean = const.tile([P, 2 * PACK], F32)
+        nc.vector.tensor_copy(out=gain_mean[:, :PACK], in_=gain_bf[:])
         neg_gain_over_n = const.tile([P, PACK], F32)
         nc.vector.tensor_scalar(
             out=neg_gain_over_n[:], in0=gain_bf[:], scalar1=-1.0 / GROUP_SIZE, scalar2=None,
             op0=ALU.mult,
         )
-        shift = const.tile([P, PACK], F32)
-        nc.vector.tensor_copy(out=shift[:], in_=shift_bf[:])
+        zero_shift = const.tile([P, 2 * PACK], F32)
+        nc.vector.memset(zero_shift[:, :PACK], 0.0)
+        nc.vector.tensor_copy(out=zero_shift[:, PACK:], in_=shift_bf[:])
         bias = const.tile([P, M_TILES], F32)
         nc.vector.tensor_copy(out=bias[:], in_=bias_bf[:])
 
@@ -317,9 +318,8 @@ def tile_multihead_attn_pa_t_kernel(tc, X, gn_w, gn_b, kqv_w, kqv_b, out):
         std = {}
 
         def moments(b):
-            neg_mean_gain[b] = stat.tile([P, PACK], F32, name="neg_mean_gain")
             nc.vector.tensor_scalar(
-                out=neg_mean_gain[b][:], in0=neg_gain_over_n[:], scalar1=total_x[b],
+                out=gain_mean[:, PACK:], in0=neg_gain_over_n[:], scalar1=total_x[b],
                 scalar2=None, op0=ALU.mult,
             )
             offset_sq = stat.tile([P, 1], F32, name="offset_sq")
@@ -347,25 +347,22 @@ def tile_multihead_attn_pa_t_kernel(tc, X, gn_w, gn_b, kqv_w, kqv_b, out):
             nc.vector.reciprocal(out=rstd[b][:], in_=std[b][:])
 
         def gain_and_shift(b):
-            a = stat.tile([P, PACK], F32, name="a")
-            nc.vector.tensor_scalar(
-                out=a[:], in0=gain[:], scalar1=rstd[b][:, 0:1], scalar2=None, op0=ALU.mult
-            )
-            c = stat.tile([P, PACK], F32, name="c")
+            a_c = stat.tile([P, 2 * PACK], F32, name="a_c")
             nc.vector.scalar_tensor_tensor(
-                out=c[:], in0=neg_mean_gain[b][:], scalar=rstd[b][:, 0:1], in1=shift[:],
+                out=a_c[:], in0=gain_mean[:], scalar=rstd[b][:, 0:1], in1=zero_shift[:],
                 op0=ALU.mult, op1=ALU.add,
             )
-            factors[b] = (a, c)
+            factors[b] = a_c
 
         def normalise(b):
-            a, c = factors[b]
+            a_c = factors[b]
             y = y_pool.tile([P, POOL, PACK, ROW_CLASS], BF16, name="y")
             for j in range(PACK):
                 nc.vector.tensor_scalar(
                     out=y[:, :, j, :].rearrange("p th (i w) -> p th i w", w=SIDE),
                     in0=x_chunk[(b, j)][:].rearrange("p (i th w) -> p th i w", th=POOL, w=SIDE),
-                    scalar1=a[:, j : j + 1], scalar2=c[:, j : j + 1], op0=ALU.mult, op1=ALU.add,
+                    scalar1=a_c[:, j : j + 1], scalar2=a_c[:, PACK + j : PACK + j + 1],
+                    op0=ALU.mult, op1=ALU.add,
                 )
             progress["chunk"] = PACK * (b + 1)
             write_loads()
@@ -463,6 +460,7 @@ def tile_multihead_attn_pa_t_kernel(tc, X, gn_w, gn_b, kqv_w, kqv_b, out):
                 if th == POOL - 1 and b + 1 < BATCH:
                     moments(b + 1)
                     if b + 2 < BATCH:
+                        later_pivot(b + 2)
                         squares(b + 2)
                     for late in range(first_scalar, POOL):
                         g[late] = regroup_on_scalar(y, late)
@@ -478,8 +476,6 @@ def tile_multihead_attn_pa_t_kernel(tc, X, gn_w, gn_b, kqv_w, kqv_b, out):
                         quantise_and_multiply(g[3], acc, 3)
                 elif th > 0:
                     quantise_and_multiply(g[th - 1], acc, th - 1)
-                if th == 2 and b + 2 < BATCH:
-                    later_pivot(b + 2)
             if b == BATCH - 1:
                 quantise_and_multiply(g[POOL - 1], acc, POOL - 1)
             acc_done = acc

@@ -134,7 +134,7 @@ def tile_multihead_attn_pa_t_kernel(tc, X, gn_w, gn_b, kqv_w, kqv_b, out):
         one = const.tile([P, 1], F32)
         nc.vector.memset(one[:], 1.0)
         table_warm = const.tile([P, 1], F32)
-        nc.scalar.activation(out=table_warm[:], in_=one[:], func=ACT.Sqrt)
+        nc.scalar.activation(out=table_warm[:], in_=one[:], func=ACT.Abs_reciprocal_sqrt)
         eps_share = {}
         for columns in (PACK, PACK + 2):
             eps_share[columns] = const.tile([P, 1], F32, name="eps_share%d" % columns)
@@ -314,8 +314,7 @@ def tile_multihead_attn_pa_t_kernel(tc, X, gn_w, gn_b, kqv_w, kqv_b, out):
             total_x[b] = part_sums[b][:, P : P + 1]
             nc.tensor.matmul(out=total_x[b], lhsT=part[:], rhs=one[:], start=True, stop=True)
 
-        neg_mean_gain = {}
-        std = {}
+        rstd = {}
 
         def moments(b):
             nc.vector.tensor_scalar(
@@ -334,17 +333,16 @@ def tile_multihead_attn_pa_t_kernel(tc, X, gn_w, gn_b, kqv_w, kqv_b, out):
                 out=sq_share[:, :columns], in_=sum_sq[b][:], func=ACT.Identity,
                 bias=eps_share[columns][:, 0:1], scale=1.0 / GROUP_SIZE, accum_out=mean_sq_eps[:],
             )
-            std[b] = stat.tile([P, 1], F32, name="std")
+            rstd[b] = stat.tile([P, 1], F32, name="rstd")
             nc.scalar.activation(
-                out=std[b][:], in_=offset_sq[:], func=ACT.Sqrt, bias=mean_sq_eps[:, 0:1], scale=-1.0
+                out=rstd[b][:], in_=offset_sq[:], func=ACT.Abs_reciprocal_sqrt,
+                bias=mean_sq_eps[:, 0:1], scale=-1.0,
             )
 
-        rstd = {}
         factors = {}
 
         def invert_std(b):
-            rstd[b] = stat.tile([P, 1], F32, name="rstd")
-            nc.vector.reciprocal(out=rstd[b][:], in_=std[b][:])
+            return None
 
         def gain_and_shift(b):
             a_c = stat.tile([P, 2 * PACK], F32, name="a_c")

@@ -379,7 +379,11 @@ def tile_multihead_attn_pa_t_kernel(tc, X, gn_w, gn_b, kqv_w, kqv_b, out):
 
         def regroup_on_vector(y, th):
             g_v = v_pool.tile([P, PIXELS], BF16, name="g_v", tag="v_out", align_bytes=64)
-            return regroup(nc.vector.tensor_copy, g_v, y, th)
+            nc.vector.tensor_copy(
+                out=g_v[:].rearrange("p (tw pair c j) -> p pair j c tw", tw=POOL, c=2, j=PACK),
+                in_=y[:, th, :, :].rearrange("p j (pair c tw) -> p pair j c tw", c=2, tw=POOL),
+            )
+            return g_v
 
         q_tiles = {}
 

@@ -1,3 +1,4 @@
+import math
 from contextlib import ExitStack
 
 import concourse.masks as masks
@@ -64,10 +65,6 @@ def tile_multihead_attn_pa_t_kernel(tc, X, gn_w, gn_b, kqv_w, kqv_b, out):
         ctx.enter_context(tc.manual_schedule())
 
         w_rows = const.tile([P, M_TILES * CHANNELS], BF16)
-        nc.scalar.dma_start(
-            out=w_rows[:].rearrange("o (m c) -> o m c", m=M_TILES),
-            in_=kqv_w.rearrange("(m o) c -> o m c", o=P),
-        )
         gain_bf = const.tile([P, PACK], BF16)
         nc.scalar.dma_start(out=gain_bf[:], in_=gn_w.rearrange("(p j) -> p j", j=PACK))
         shift_bf = const.tile([P, PACK], BF16)
@@ -111,19 +108,25 @@ def tile_multihead_attn_pa_t_kernel(tc, X, gn_w, gn_b, kqv_w, kqv_b, out):
                 x2_tile[i] = x2
 
         load_order = [("chunk", k) for k in range(PACK)]
+        load_order.append(("weights", 0))
         for k in range(len(x2_list) - LOADS):
             load_order.extend([("copy", k), ("chunk", PACK + k)])
         load_order.extend([("chunk", PACK * (BATCH - 1) + j) for j in range(PACK)])
         load_order.extend([("copy", len(x2_list) - LOADS + h) for h in range(LOADS)])
-        progress = {"loads": 0, "copy": 0, "chunk": 0}
-        room = {"copy": X2_SLOTS, "chunk": X_SLOTS}
+        progress = {"loads": 0, "copy": 0, "chunk": 0, "weights": 0}
+        room = {"copy": X2_SLOTS, "chunk": X_SLOTS, "weights": 1}
 
         def write_loads():
             for n in range(progress["loads"], len(load_order)):
                 kind, k = load_order[n]
                 if k >= room[kind] + progress[kind]:
                     return
-                if kind == "copy":
+                if kind == "weights":
+                    nc.sync.dma_start(
+                        out=w_rows[:].rearrange("o (m c) -> o m c", m=M_TILES),
+                        in_=kqv_w.rearrange("(m o) c -> o m c", o=P),
+                    )
+                elif kind == "copy":
                     load_x2(k, 1)
                 else:
                     load_chunks(k, 1)
@@ -136,7 +139,7 @@ def tile_multihead_attn_pa_t_kernel(tc, X, gn_w, gn_b, kqv_w, kqv_b, out):
         table_warm = const.tile([P, 1], F32)
         nc.scalar.activation(out=table_warm[:], in_=one[:], func=ACT.Abs_reciprocal_sqrt)
         eps_share = {}
-        for columns in (PACK, PACK + 2):
+        for columns in (PACK, PACK + 3):
             eps_share[columns] = const.tile([P, 1], F32, name="eps_share%d" % columns)
             nc.vector.memset(eps_share[columns][:], EPS / columns)
 
@@ -155,9 +158,6 @@ def tile_multihead_attn_pa_t_kernel(tc, X, gn_w, gn_b, kqv_w, kqv_b, out):
 
         w_words = w_rows[:].bitcast(F32).rearrange("o (m p u) -> o m u p", m=M_TILES, u=2)
         w_t = psum_w.tile([P, 2, OUT_CH], F32)
-        for m in range(M_TILES):
-            for u in range(2):
-                nc.tensor.transpose(w_t[:, u, m * P : (m + 1) * P], w_words[:, m, u, :], identity[:])
         w_grouped = const.tile([P, OUT_CH * PACK], BF16, align_bytes=64)
         w_codes = const.tile([P, OUT_CH], U32, align_bytes=64)
         w_scales = const.tile([P, OUT_CH], U8, align_bytes=64)
@@ -211,7 +211,8 @@ def tile_multihead_attn_pa_t_kernel(tc, X, gn_w, gn_b, kqv_w, kqv_b, out):
                 square_on_scalar(b, j, 0, PIXELS, j)
 
         sum_x0 = const.tile([P, PACK + 1], F32)
-        sum_sq0 = const.tile([P, PACK + 2], F32)
+        sum_sq0 = const.tile([P, PACK + 3], F32)
+        mean_var = const.tile([P, 2], F32)
         sum_sq[0] = sum_sq0
         bn_out = const.tile([P, BN_VALUES // BN_WIDTH, 6], F32)
         ident_bf = const.tile([P, P], BF16)
@@ -241,10 +242,6 @@ def tile_multihead_attn_pa_t_kernel(tc, X, gn_w, gn_b, kqv_w, kqv_b, out):
         for j in range(PACK):
             if j == 0:
                 square_on_scalar(0, 0, 0, HEAD_FIRST, PACK)
-                nc.scalar.copy(
-                    out=w_grouped[:].bitcast(F32).rearrange("p (o u) -> p o u", u=2),
-                    in_=w_t[:].rearrange("p u o -> p o u"),
-                )
                 square_on_scalar(0, 0, HEAD_FIRST, HEAD_SCALAR[0], 0)
             else:
                 square_on_scalar(0, j, 0, HEAD_SCALAR[j], j)
@@ -256,6 +253,7 @@ def tile_multihead_attn_pa_t_kernel(tc, X, gn_w, gn_b, kqv_w, kqv_b, out):
             if j == 0:
                 sum_on_vector(x_chunk[(0, 0)], PIVOT_PIXELS, HEAD_SCALAR[0], sum_x0[:, 4:5])
             if j == PACK - 1:
+                nc.vector.bn_aggr(out=mean_var[:], in_=bn_out[:].rearrange("p i s -> p (i s)"))
                 sum_on_vector(x_chunk[(0, j)], HEAD_FOLD_3, HEAD_SCALAR[j], sum_x0[:, 1:2])
         for n in range(len(fold_list)):
             j, c = fold_list[n]
@@ -263,26 +261,25 @@ def tile_multihead_attn_pa_t_kernel(tc, X, gn_w, gn_b, kqv_w, kqv_b, out):
                 out=folded[:, :P], lhsT=ident_bf[:], rhs=x_chunk[(0, j)][:, c * P : (c + 1) * P],
                 start=(n == 0), stop=(n == len(fold_list) - 1),
             )
-        later_pivot(1)
+        for m in range(M_TILES):
+            for u in range(2):
+                nc.tensor.transpose(w_t[:, u, m * P : (m + 1) * P], w_words[:, m, u, :], identity[:])
+        off_pivot = const.tile([P, 1], F32)
+        nc.vector.tensor_scalar(
+            out=off_pivot[:], in0=mean_var[:, 0:1], scalar1=neg_pivot[0][:, 0:1],
+            scalar2=math.sqrt(BN_VALUES), op0=ALU.add, op1=ALU.mult,
+        )
         nc.vector.reduce_sum(out=sum_x0[:, 2:3], in_=folded[:, :P], axis=AXIS.X)
-        mean_var = const.tile([P, 2], F32)
-        nc.vector.bn_aggr(out=mean_var[:], in_=bn_out[:].rearrange("p i s -> p (i s)"))
         nc.vector.tensor_scalar(
             out=sum_x0[:, 3:4], in0=mean_var[:, 0:1], scalar1=float(BN_VALUES), scalar2=None,
             op0=ALU.mult,
         )
-        off_pivot = const.tile([P, 1], F32)
         nc.vector.tensor_scalar(
-            out=off_pivot[:], in0=mean_var[:, 0:1], scalar1=neg_pivot[0][:, 0:1], scalar2=None,
-            op0=ALU.add,
-        )
-        mean_sq_off = const.tile([P, 1], F32)
-        nc.vector.scalar_tensor_tensor(
-            out=mean_sq_off[:], in0=off_pivot[:], scalar=off_pivot[:, 0:1], in1=mean_var[:, 1:2],
-            op0=ALU.mult, op1=ALU.add,
+            out=sum_sq0[:, PACK + 1 : PACK + 2], in0=mean_var[:, 1:2], scalar1=float(BN_VALUES),
+            scalar2=None, op0=ALU.mult,
         )
         nc.vector.tensor_scalar(
-            out=sum_sq0[:, PACK + 1 : PACK + 2], in0=mean_sq_off[:], scalar1=float(BN_VALUES),
+            out=sum_sq0[:, PACK + 2 : PACK + 3], in0=off_pivot[:], scalar1=off_pivot[:, 0:1],
             scalar2=None, op0=ALU.mult,
         )
         total_x0 = const.tile([P, 1], F32)
@@ -327,7 +324,7 @@ def tile_multihead_attn_pa_t_kernel(tc, X, gn_w, gn_b, kqv_w, kqv_b, out):
                 scale=1.0 / GROUP_SIZE,
             )
             columns = sum_sq[b][:].shape[1]
-            sq_share = stat.tile([P, PACK + 2], F32, name="sq_share")
+            sq_share = stat.tile([P, PACK + 3], F32, name="sq_share")
             mean_sq_eps = stat.tile([P, 1], F32, name="mean_sq_eps")
             nc.scalar.activation(
                 out=sq_share[:, :columns], in_=sum_sq[b][:], func=ACT.Identity,
@@ -430,9 +427,14 @@ def tile_multihead_attn_pa_t_kernel(tc, X, gn_w, gn_b, kqv_w, kqv_b, out):
             nc.sync.dma_start(out=out[b, P:OUT_CH].rearrange("o i jj -> o (i jj)"), in_=res1[:])
 
         moments(0)
+        later_pivot(1)
         squares(1)
         for i in range(LOADS):
             sum_on_tensor(i)
+        nc.vector.tensor_copy(
+            out=w_grouped[:].bitcast(F32).rearrange("p (o u) -> p o u", u=2),
+            in_=w_t[:].rearrange("p u o -> p o u"),
+        )
         quantise_weights()
         invert_std(0)
         gain_and_shift(0)
@@ -449,7 +451,7 @@ def tile_multihead_attn_pa_t_kernel(tc, X, gn_w, gn_b, kqv_w, kqv_b, out):
             for th in range(POOL):
                 if th < first_scalar:
                     g[th] = regroup_on_vector(y, th)
-                if th == 2 and b > 0:
+                if th == 2 and b == BATCH - 1:
                     for m in range(M_TILES):
                         leave_on_scalar(b - 1, acc_done, m)
                 if th == 2 and b + 1 < BATCH:
@@ -463,6 +465,10 @@ def tile_multihead_attn_pa_t_kernel(tc, X, gn_w, gn_b, kqv_w, kqv_b, out):
                     moments(b + 1)
                     if b + 2 < BATCH:
                         later_pivot(b + 2)
+                    if b > 0:
+                        for m in range(M_TILES):
+                            leave_on_scalar(b - 1, acc_done, m)
+                    if b + 2 < BATCH:
                         squares(b + 2)
                     for late in range(first_scalar, POOL):
                         g[late] = regroup_on_scalar(y, late)
@@ -479,7 +485,8 @@ def tile_multihead_attn_pa_t_kernel(tc, X, gn_w, gn_b, kqv_w, kqv_b, out):
                 elif th > 0:
                     quantise_and_multiply(g[th - 1], acc, th - 1)
             if b == BATCH - 1:
-                quantise_and_multiply(g[POOL - 1], acc, POOL - 1)
+                for piece in range(4):
+                    quantise_and_multiply(g[POOL - 1], acc, POOL - 1, piece * (POOL // 4), POOL // 4)
             acc_done = acc
         leave_on_scalar(BATCH - 1, acc_done, 0)
         leave_on_vector(BATCH - 1, acc_done)

@@ -313,7 +313,8 @@ def tile_multihead_attn_pa_t_kernel(tc, X, gn_w, gn_b, kqv_w, kqv_b, out):
 
         rstd = {}
 
-        def moments(b):
+        def moments(b, fillers=()):
+            fillers = list(fillers)
             nc.vector.tensor_scalar(
                 out=gain_mean[:, PACK:], in0=neg_gain_over_n[:], scalar1=total_x[b],
                 scalar2=None, op0=ALU.mult,
@@ -323,6 +324,8 @@ def tile_multihead_attn_pa_t_kernel(tc, X, gn_w, gn_b, kqv_w, kqv_b, out):
                 out=offset_sq[:], in_=total_x[b], func=ACT.Square, bias=neg_pivot[b][:, 0:1],
                 scale=1.0 / GROUP_SIZE,
             )
+            if len(fillers) > 0:
+                fillers[0]()
             columns = sum_sq[b][:].shape[1]
             sq_share = stat.tile([P, PACK + 3], F32, name="sq_share")
             mean_sq_eps = stat.tile([P, 1], F32, name="mean_sq_eps")
@@ -330,6 +333,8 @@ def tile_multihead_attn_pa_t_kernel(tc, X, gn_w, gn_b, kqv_w, kqv_b, out):
                 out=sq_share[:, :columns], in_=sum_sq[b][:], func=ACT.Identity,
                 bias=eps_share[columns][:, 0:1], scale=1.0 / GROUP_SIZE, accum_out=mean_sq_eps[:],
             )
+            if len(fillers) > 1:
+                fillers[1]()
             rstd[b] = stat.tile([P, 1], F32, name="rstd")
             nc.scalar.activation(
                 out=rstd[b][:], in_=offset_sq[:], func=ACT.Abs_reciprocal_sqrt,
@@ -462,12 +467,15 @@ def tile_multihead_attn_pa_t_kernel(tc, X, gn_w, gn_b, kqv_w, kqv_b, out):
                     sum_on_tensor(2 * LOADS + 2 * th)
                     sum_on_tensor(2 * LOADS + 2 * th + 1)
                 if th == POOL - 1 and b + 1 < BATCH:
-                    moments(b + 1)
+                    fillers = []
                     if b + 2 < BATCH:
-                        later_pivot(b + 2)
+                        fillers.append(lambda: later_pivot(b + 2))
                     if b > 0:
-                        for m in range(M_TILES):
-                            leave_on_scalar(b - 1, acc_done, m)
+                        fillers.append(lambda: leave_on_scalar(b - 1, acc_done, 0))
+                        fillers.append(lambda: leave_on_scalar(b - 1, acc_done, 1))
+                    moments(b + 1, fillers[:2])
+                    for filler in fillers[2:]:
+                        filler()
                     if b + 2 < BATCH:
                         squares(b + 2)
                     for late in range(first_scalar, POOL):

import math
from contextlib import ExitStack

import concourse.masks as masks
import concourse.mybir as mybir

F32 = mybir.dt.float32
BF16 = mybir.dt.bfloat16
U32 = mybir.dt.uint32
U8 = mybir.dt.uint8
FP8X4 = mybir.dt.float8_e4m3fn_x4
ALU = mybir.AluOpType
ACT = mybir.ActivationFunctionType
AXIS = mybir.AxisListType

P = 128
PACK = 4
BATCH = 4
CHANNELS = P * PACK
OUT_CH = 256
M_TILES = OUT_CH // P
SIDE = 64
PIXELS = SIDE * SIDE
POOL = 4
CELLS = (SIDE // POOL) * (SIDE // POOL)
ROW_CLASS = POOL * CELLS
GROUP_SIZE = PACK * PIXELS
EPS = 1e-5
PIVOT_PIXELS = 256
X_SLOTS = 8
PE_SUM_FROM = 1
SLABS = 8
RUN = 2048
PARTS_OF_GROUP = 8
CLASSES = 16
SLABS_PER_LOAD = 2
X2_SLOTS = 4
SCALAR_CLASSES = (0, 0, 1, 2)
HEAD_SCALAR = (2560, 2560, 3072, 3072)
HEAD_FOLD_3 = 512
HEAD_FIRST = 1024
BN_WIDTH = 512
BN_VALUES = PACK * PIXELS - sum(HEAD_SCALAR)

FLOPS = 2 * BATCH * OUT_CH * CHANNELS * PIXELS


def tile_multihead_attn_pa_t_kernel(tc, X, gn_w, gn_b, kqv_w, kqv_b, out):
    nc = tc.nc
    with ExitStack() as ctx:
        const = ctx.enter_context(tc.tile_pool(name="const", bufs=1))
        x_pool = ctx.enter_context(tc.tile_pool(name="x", bufs=X_SLOTS))
        x2_pool = ctx.enter_context(tc.tile_pool(name="x2", bufs=X2_SLOTS))
        junk_pool = ctx.enter_context(tc.tile_pool(name="junk", bufs=1))
        part_pool = ctx.enter_context(tc.tile_pool(name="part", bufs=2))
        y_pool = ctx.enter_context(tc.tile_pool(name="y", bufs=2))
        v_pool = ctx.enter_context(tc.tile_pool(name="v_out", bufs=3))
        g_s_pool = ctx.enter_context(tc.tile_pool(name="g_s", bufs=2))
        q_pool = ctx.enter_context(tc.tile_pool(name="q", bufs=3))
        stat = ctx.enter_context(tc.tile_pool(name="stat", bufs=BATCH))
        res_pool = ctx.enter_context(tc.tile_pool(name="res", bufs=4))
        psum_w = ctx.enter_context(tc.psum_pool(name="psum_w", bufs=1))
        psum = ctx.enter_context(tc.psum_pool(name="psum", bufs=2))
        psum_s = ctx.enter_context(tc.psum_pool(name="psum_s", bufs=2))
        ctx.enter_context(tc.manual_schedule())

        w_rows = const.tile([P, M_TILES * CHANNELS], BF16)
        gain_bf = const.tile([P, PACK], BF16)
        nc.scalar.dma_start(out=gain_bf[:], in_=gn_w.rearrange("(p j) -> p j", j=PACK))
        shift_bf = const.tile([P, PACK], BF16)
        nc.scalar.dma_start(out=shift_bf[:], in_=gn_b.rearrange("(p j) -> p j", j=PACK))
        bias_bf = const.tile([P, M_TILES], BF16)
        with nc.allow_non_contiguous_dma(reason="256 bias values, one output channel a partition"):
            nc.scalar.dma_start(out=bias_bf[:], in_=kqv_b.rearrange("(m o) -> o m", o=P))

        x_chunk = {}

        def load_chunks(first, count):
            for k in range(first, min(first + count, BATCH * PACK)):
                b, j = divmod(k, PACK)
                pixels = X[b].rearrange("(p j) h w -> p j (h w)", j=PACK)[:, j, :]
                x_bj = x_pool.tile([P, PIXELS], BF16, name="x_bj")
                cuts = [0, PIXELS]
                if j == 0:
                    cuts = [0, PIVOT_PIXELS, PIXELS]
                if k == 0:
                    cuts = [0, PIVOT_PIXELS, HEAD_FIRST, PIXELS]
                for n in range(len(cuts) - 1):
                    nc.sync.dma_start(
                        out=x_bj[:, cuts[n] : cuts[n + 1]], in_=pixels[:, cuts[n] : cuts[n + 1]]
                    )
                x_chunk[(b, j)] = x_bj

        LOADS = SLABS // SLABS_PER_LOAD
        x2_list = [(b, h) for b in range(PE_SUM_FROM, BATCH) for h in range(LOADS)]
        x2_tile = {}

        def load_x2(first, count):
            for i in range(first, min(first + count, len(x2_list))):
                b, h = x2_list[i]
                slabs = X[b].rearrange("c h w -> (c h w)").rearrange(
                    "(s k e) -> k s e", s=SLABS, k=P
                )
                x2 = x2_pool.tile([P, SLABS_PER_LOAD, RUN], BF16, name="x2")
                nc.sync.dma_start(
                    out=x2[:], in_=slabs[:, h * SLABS_PER_LOAD : (h + 1) * SLABS_PER_LOAD, :]
                )
                x2_tile[i] = x2

        load_order = [("chunk", k) for k in range(PACK)]
        load_order.append(("weights", 0))
        for k in range(len(x2_list) - LOADS):
            load_order.extend([("copy", k), ("chunk", PACK + k)])
        load_order.extend([("chunk", PACK * (BATCH - 1) + j) for j in range(PACK)])
        load_order.extend([("copy", len(x2_list) - LOADS + h) for h in range(LOADS)])
        progress = {"loads": 0, "copy": 0, "chunk": 0, "weights": 0}
        room = {"copy": X2_SLOTS, "chunk": X_SLOTS, "weights": 1}

        def write_loads():
            for n in range(progress["loads"], len(load_order)):
                kind, k = load_order[n]
                if k >= room[kind] + progress[kind]:
                    return
                if kind == "weights":
                    nc.sync.dma_start(
                        out=w_rows[:].rearrange("o (m c) -> o m c", m=M_TILES),
                        in_=kqv_w.rearrange("(m o) c -> o m c", o=P),
                    )
                elif kind == "copy":
                    load_x2(k, 1)
                else:
                    load_chunks(k, 1)
                progress["loads"] = n + 1

        write_loads()

        one = const.tile([P, 1], F32)
        nc.vector.memset(one[:], 1.0)
        table_warm = const.tile([P, 1], F32)
        nc.scalar.activation(out=table_warm[:], in_=one[:], func=ACT.Abs_reciprocal_sqrt)
        eps_share = {}
        for columns in (PACK, PACK + 3):
            eps_share[columns] = const.tile([P, 1], F32, name="eps_share%d" % columns)
            nc.vector.memset(eps_share[columns][:], EPS / columns)

        class_mask = const.tile([P, CLASSES], BF16)
        nc.gpsimd.memset(class_mask[:], 1.0)
        nc.gpsimd.affine_select(
            out=class_mask[:], in_=class_mask[:], compare_op=ALU.is_ge, fill=0.0, base=0,
            pattern=[[-PARTS_OF_GROUP, CLASSES]], channel_multiplier=1,
        )
        nc.gpsimd.affine_select(
            out=class_mask[:], in_=class_mask[:], compare_op=ALU.is_ge, fill=0.0,
            base=PARTS_OF_GROUP - 1, pattern=[[PARTS_OF_GROUP, CLASSES]], channel_multiplier=-1,
        )
        identity = const.tile([P, P], F32)
        masks.make_identity(nc, identity[:])

        w_words = w_rows[:].bitcast(F32).rearrange("o (m p u) -> o m u p", m=M_TILES, u=2)
        w_t = psum_w.tile([P, 2, OUT_CH], F32)
        w_grouped = const.tile([P, OUT_CH * PACK], BF16, align_bytes=64)
        w_codes = const.tile([P, OUT_CH], U32, align_bytes=64)
        w_scales = const.tile([P, OUT_CH], U8, align_bytes=64)

        def quantise_weights():
            nc.vector.quantize_mx(
                out=w_codes[:].bitcast(FP8X4), scales=w_scales[:], in_=w_grouped[:]
            )

        sum_sq = {}
        neg_pivot = {}
        total_x = {}

        def sum_on_vector(x_bj, lo, hi, accum):
            unread_v = v_pool.tile([P, PIXELS], BF16, name="unread_v", tag="v_out", align_bytes=64)
            nc.vector.tensor_scalar(
                out=unread_v[:, lo:hi], in0=x_bj[:, lo:hi], scalar1=1.0, scalar2=None,
                op0=ALU.mult, op1=ALU.add, accum_out=accum,
            )

        def pivot(b, sum_pivot):
            neg_pivot[b] = stat.tile([P, 1], F32, name="neg_pivot")
            junk = junk_pool.tile([P, PIVOT_PIXELS], BF16, name="junk")
            nc.vector.tensor_scalar(
                out=junk[:], in0=x_chunk[(b, 0)][:, :PIVOT_PIXELS], scalar1=1.0,
                scalar2=None, op0=ALU.mult, op1=ALU.add, accum_out=sum_pivot,
            )
            nc.vector.tensor_scalar(
                out=neg_pivot[b][:], in0=sum_pivot, scalar1=-1.0 / PIVOT_PIXELS,
                scalar2=None, op0=ALU.mult,
            )

        def later_pivot(b):
            neg_pivot[b] = stat.tile([P, 1], F32, name="neg_pivot")
            junk_s = junk_pool.tile([P, PIVOT_PIXELS], BF16, name="junk_s")
            nc.scalar.activation(
                out=junk_s[:], in_=x_chunk[(b, 0)][:, :PIVOT_PIXELS], func=ACT.Identity,
                scale=-1.0 / PIVOT_PIXELS, accum_out=neg_pivot[b][:],
            )

        def square_on_scalar(b, j, first, end, column):
            unread_s = g_s_pool.tile([P, PIXELS], BF16, name="unread_s", tag="g_s", align_bytes=64)
            nc.scalar.activation(
                out=unread_s[:, first:end], in_=x_chunk[(b, j)][:, first:end], func=ACT.Square,
                bias=neg_pivot[b][:, 0:1], scale=1.0, accum_out=sum_sq[b][:, column : column + 1],
            )

        def squares(b):
            sum_sq[b] = stat.tile([P, PACK], F32, name="sum_sq")
            for j in range(PACK):
                square_on_scalar(b, j, 0, PIXELS, j)

        sum_x0 = const.tile([P, PACK + 1], F32)
        sum_sq0 = const.tile([P, PACK + 3], F32)
        mean_var = const.tile([P, 2], F32)
        sum_sq[0] = sum_sq0
        bn_out = const.tile([P, BN_VALUES // BN_WIDTH, 6], F32)
        ident_bf = const.tile([P, P], BF16)
        masks.make_identity(nc, ident_bf[:])
        folded = psum_s.tile([P, 512], F32, name="part_sums")
        fold_list = [
            (j, c)
            for j in range(1, PACK)
            for c in range((HEAD_SCALAR[j] if j < PACK - 1 else HEAD_FOLD_3) // P)
        ]

        pivot(0, sum_x0[:, 0:1])
        gain_mean = const.tile([P, 2 * PACK], F32)
        nc.vector.tensor_copy(out=gain_mean[:, :PACK], in_=gain_bf[:])
        neg_gain_over_n = const.tile([P, PACK], F32)
        nc.vector.tensor_scalar(
            out=neg_gain_over_n[:], in0=gain_bf[:], scalar1=-1.0 / GROUP_SIZE, scalar2=None,
            op0=ALU.mult,
        )
        zero_shift = const.tile([P, 2 * PACK], F32)
        nc.vector.memset(zero_shift[:, :PACK], 0.0)
        nc.vector.tensor_copy(out=zero_shift[:, PACK:], in_=shift_bf[:])
        bias = const.tile([P, M_TILES], F32)
        nc.vector.tensor_copy(out=bias[:], in_=bias_bf[:])

        pieces = 0
        for j in range(PACK):
            if j == 0:
                square_on_scalar(0, 0, 0, HEAD_FIRST, PACK)
                square_on_scalar(0, 0, HEAD_FIRST, HEAD_SCALAR[0], 0)
            else:
                square_on_scalar(0, j, 0, HEAD_SCALAR[j], j)
            for first in range(HEAD_SCALAR[j], PIXELS, BN_WIDTH):
                nc.vector.bn_stats(
                    out=bn_out[:, pieces, :], in_=x_chunk[(0, j)][:, first : first + BN_WIDTH]
                )
                pieces = pieces + 1
            if j == 0:
                sum_on_vector(x_chunk[(0, 0)], PIVOT_PIXELS, HEAD_SCALAR[0], sum_x0[:, 4:5])
            if j == PACK - 1:
                nc.vector.bn_aggr(out=mean_var[:], in_=bn_out[:].rearrange("p i s -> p (i s)"))
                sum_on_vector(x_chunk[(0, j)], HEAD_FOLD_3, HEAD_SCALAR[j], sum_x0[:, 1:2])
        for n in range(len(fold_list)):
            j, c = fold_list[n]
            nc.tensor.matmul(
                out=folded[:, :P], lhsT=ident_bf[:], rhs=x_chunk[(0, j)][:, c * P : (c + 1) * P],
                start=(n == 0), stop=(n == len(fold_list) - 1),
            )
        for m in range(M_TILES):
            for u in range(2):
                nc.tensor.transpose(w_t[:, u, m * P : (m + 1) * P], w_words[:, m, u, :], identity[:])
        off_pivot = const.tile([P, 1], F32)
        nc.vector.tensor_scalar(
            out=off_pivot[:], in0=mean_var[:, 0:1], scalar1=neg_pivot[0][:, 0:1],
            scalar2=math.sqrt(BN_VALUES), op0=ALU.add, op1=ALU.mult,
        )
        nc.vector.reduce_sum(out=sum_x0[:, 2:3], in_=folded[:, :P], axis=AXIS.X)
        nc.vector.tensor_scalar(
            out=sum_x0[:, 3:4], in0=mean_var[:, 0:1], scalar1=float(BN_VALUES), scalar2=None,
            op0=ALU.mult,
        )
        nc.vector.tensor_scalar(
            out=sum_sq0[:, PACK + 1 : PACK + 2], in0=mean_var[:, 1:2], scalar1=float(BN_VALUES),
            scalar2=None, op0=ALU.mult,
        )
        nc.vector.tensor_scalar(
            out=sum_sq0[:, PACK + 2 : PACK + 3], in0=off_pivot[:], scalar1=off_pivot[:, 0:1],
            scalar2=None, op0=ALU.mult,
        )
        total_x0 = const.tile([P, 1], F32)
        nc.vector.reduce_sum(out=total_x0[:], in_=sum_x0[:], axis=AXIS.X)
        total_x[0] = total_x0[:]

        part_sums = {}

        def sum_on_tensor(i):
            b, h = x2_list[i]
            if h == 0:
                part_sums[b] = psum_s.tile([P, 512], F32, name="part_sums")
            for s in range(SLABS_PER_LOAD):
                first = (h * SLABS_PER_LOAD + s) * CLASSES
                for c in range(RUN // P):
                    nc.tensor.matmul(
                        out=part_sums[b][:, first : first + CLASSES],
                        lhsT=x2_tile[i][:, s, c * P : (c + 1) * P],
                        rhs=class_mask[:],
                        start=(c == 0),
                        stop=(c == RUN // P - 1),
                    )
            progress["copy"] = i + 1
            write_loads()

        def gather_total(b):
            part = part_pool.tile([P, P], F32, name="part")
            nc.vector.tensor_copy(out=part[:], in_=part_sums[b][:, :P])
            total_x[b] = part_sums[b][:, P : P + 1]
            nc.tensor.matmul(out=total_x[b], lhsT=part[:], rhs=one[:], start=True, stop=True)

        rstd = {}

        def moments(b, fillers=()):
            fillers = list(fillers)
            nc.vector.tensor_scalar(
                out=gain_mean[:, PACK:], in0=neg_gain_over_n[:], scalar1=total_x[b],
                scalar2=None, op0=ALU.mult,
            )
            offset_sq = stat.tile([P, 1], F32, name="offset_sq")
            nc.scalar.activation(
                out=offset_sq[:], in_=total_x[b], func=ACT.Square, bias=neg_pivot[b][:, 0:1],
                scale=1.0 / GROUP_SIZE,
            )
            if len(fillers) > 0:
                fillers[0]()
            columns = sum_sq[b][:].shape[1]
            sq_share = stat.tile([P, PACK + 3], F32, name="sq_share")
            mean_sq_eps = stat.tile([P, 1], F32, name="mean_sq_eps")
            nc.scalar.activation(
                out=sq_share[:, :columns], in_=sum_sq[b][:], func=ACT.Identity,
                bias=eps_share[columns][:, 0:1], scale=1.0 / GROUP_SIZE, accum_out=mean_sq_eps[:],
            )
            if len(fillers) > 1:
                fillers[1]()
            rstd[b] = stat.tile([P, 1], F32, name="rstd")
            nc.scalar.activation(
                out=rstd[b][:], in_=offset_sq[:], func=ACT.Abs_reciprocal_sqrt,
                bias=mean_sq_eps[:, 0:1], scale=-1.0,
            )

        factors = {}

        def invert_std(b):
            return None

        def gain_and_shift(b):
            a_c = stat.tile([P, 2 * PACK], F32, name="a_c")
            nc.vector.scalar_tensor_tensor(
                out=a_c[:], in0=gain_mean[:], scalar=rstd[b][:, 0:1], in1=zero_shift[:],
                op0=ALU.mult, op1=ALU.add,
            )
            factors[b] = a_c

        def normalise(b):
            a_c = factors[b]
            y = y_pool.tile([P, POOL, PACK, ROW_CLASS], BF16, name="y")
            for j in range(PACK):
                nc.vector.tensor_scalar(
                    out=y[:, :, j, :].rearrange("p th (i w) -> p th i w", w=SIDE),
                    in0=x_chunk[(b, j)][:].rearrange("p (i th w) -> p th i w", th=POOL, w=SIDE),
                    scalar1=a_c[:, j : j + 1], scalar2=a_c[:, PACK + j : PACK + j + 1],
                    op0=ALU.mult, op1=ALU.add,
                )
            progress["chunk"] = PACK * (b + 1)
            write_loads()
            return y

        def regroup(copy, g, y, th):
            copy(
                out=g[:].rearrange("p (tw cell j) -> p cell j tw", tw=POOL, j=PACK),
                in_=y[:, th, :, :].rearrange("p j (cell tw) -> p cell j tw", tw=POOL),
            )
            return g

        def regroup_on_scalar(y, th):
            g_s = g_s_pool.tile([P, PIXELS], BF16, name="g_s", tag="g_s", align_bytes=64)
            return regroup(nc.scalar.copy, g_s, y, th)

        def regroup_on_vector(y, th):
            g_v = v_pool.tile([P, PIXELS], BF16, name="g_v", tag="v_out", align_bytes=64)
            nc.vector.tensor_copy(
                out=g_v[:].rearrange("p (tw pair c j) -> p pair j c tw", tw=POOL, c=2, j=PACK),
                in_=y[:, th, :, :].rearrange("p j (pair c tw) -> p pair j c tw", c=2, tw=POOL),
            )
            return g_v

        q_tiles = {}

        def quantise_and_multiply(g, acc, th, first_plane=0, planes=POOL):
            if first_plane == 0:
                codes = q_pool.tile([P, POOL * CELLS], U32, name="codes", align_bytes=64)
                scales = q_pool.tile([P, POOL * CELLS], U8, name="scales", align_bytes=64)
                q_tiles[th] = (codes, scales)
            codes, scales = q_tiles[th]
            part = slice(first_plane * CELLS, (first_plane + planes) * CELLS)
            nc.vector.quantize_mx(
                out=codes[:, part].bitcast(FP8X4), scales=scales[:, part],
                in_=g[:, first_plane * CELLS * PACK : (first_plane + planes) * CELLS * PACK],
            )
            for m in range(M_TILES):
                for tw in range(first_plane, first_plane + planes):
                    plane = slice(tw * CELLS, (tw + 1) * CELLS)
                    nc.tensor.matmul_mx(
                        out=acc[m][:],
                        lhsT=w_codes[:, m * P : (m + 1) * P].bitcast(FP8X4),
                        lhsT_scale=w_scales[:, m * P : (m + 1) * P],
                        rhs=codes[:, plane].bitcast(FP8X4),
                        rhs_scale=scales[:, plane],
                        start=(th == 0 and tw == 0),
                        stop=(th == POOL - 1 and tw == POOL - 1),
                    )

        def leave_on_scalar(b, acc, m):
            res0 = res_pool.tile([P, CELLS], F32, name="res0")
            nc.scalar.activation(
                out=res0[:], in_=acc[m][:], func=ACT.Identity, bias=bias[:, m : m + 1],
                scale=1.0 / (POOL * POOL),
            )
            nc.sync.dma_start(
                out=out[b, m * P : (m + 1) * P].rearrange("o i jj -> o (i jj)"), in_=res0[:]
            )

        def leave_on_vector(b, acc):
            res1 = res_pool.tile([P, CELLS], F32, name="res1")
            nc.vector.tensor_scalar(
                out=res1[:], in0=acc[1][:], scalar1=1.0 / (POOL * POOL), scalar2=bias[:, 1:2],
                op0=ALU.mult, op1=ALU.add,
            )
            nc.sync.dma_start(out=out[b, P:OUT_CH].rearrange("o i jj -> o (i jj)"), in_=res1[:])

        moments(0)
        later_pivot(1)
        squares(1)
        for i in range(LOADS):
            sum_on_tensor(i)
        nc.vector.tensor_copy(
            out=w_grouped[:].bitcast(F32).rearrange("p (o u) -> p o u", u=2),
            in_=w_t[:].rearrange("p u o -> p o u"),
        )
        quantise_weights()
        invert_std(0)
        gain_and_shift(0)
        y_next = normalise(0)
        acc_done = None
        for b in range(BATCH):
            y = y_next
            first_scalar = POOL - SCALAR_CLASSES[b]
            g = {}
            if b == BATCH - 1:
                for th in range(first_scalar, POOL):
                    g[th] = regroup_on_scalar(y, th)
            acc = [psum.tile([P, CELLS], F32, name="acc%d" % m) for m in range(M_TILES)]
            for th in range(POOL):
                if th < first_scalar:
                    g[th] = regroup_on_vector(y, th)
                if th == 2 and b == BATCH - 1:
                    for m in range(M_TILES):
                        leave_on_scalar(b - 1, acc_done, m)
                if th == 2 and b + 1 < BATCH:
                    gather_total(b + 1)
                if LOADS <= POOL * b + th + 2 < 2 * LOADS:
                    sum_on_tensor(POOL * b + th + 2)
                if b == BATCH - 2 and th < 2:
                    sum_on_tensor(2 * LOADS + 2 * th)
                    sum_on_tensor(2 * LOADS + 2 * th + 1)
                if th == POOL - 1 and b + 1 < BATCH:
                    fillers = []
                    if b + 2 < BATCH:
                        fillers.append(lambda: later_pivot(b + 2))
                    if b > 0:
                        fillers.append(lambda: leave_on_scalar(b - 1, acc_done, 0))
                        fillers.append(lambda: leave_on_scalar(b - 1, acc_done, 1))
                    moments(b + 1, fillers[:2])
                    for filler in fillers[2:]:
                        filler()
                    if b + 2 < BATCH:
                        squares(b + 2)
                    for late in range(first_scalar, POOL):
                        g[late] = regroup_on_scalar(y, late)
                    invert_std(b + 1)
                    quantise_and_multiply(g[2], acc, 2)
                    gain_and_shift(b + 1)
                    if first_scalar == POOL:
                        quantise_and_multiply(g[3], acc, 3, 0, 2)
                    y_next = normalise(b + 1)
                    if first_scalar == POOL:
                        quantise_and_multiply(g[3], acc, 3, 2, 2)
                    else:
                        quantise_and_multiply(g[3], acc, 3)
                elif th > 0:
                    quantise_and_multiply(g[th - 1], acc, th - 1)
            if b == BATCH - 1:
                for piece in range(4):
                    quantise_and_multiply(g[POOL - 1], acc, POOL - 1, piece * (POOL // 4), POOL // 4)
            acc_done = acc
        leave_on_scalar(BATCH - 1, acc_done, 0)
        leave_on_vector(BATCH - 1, acc_done)
